import numpy as np
import ml_dtypes


def mxq(x, axis, fmt="e4m3"):
    dtype, down = {"e4m3": (ml_dtypes.float8_e4m3fn, 7), "e5m2": (ml_dtypes.float8_e5m2, 14)}[fmt]
    v = np.moveaxis(np.asarray(x, np.float32).astype(ml_dtypes.bfloat16).astype(np.float64), axis, -1)
    blocks = v.reshape(v.shape[:-1] + (-1, 32))
    amax = np.abs(blocks).max(-1, keepdims=True)
    byte = np.maximum(np.where(amax > 0, np.frexp(amax)[1] - 1 + 127, 0) - down, 1)
    scale = np.exp2(byte - 127.0)
    codes = (blocks / scale).astype(np.float32).astype(dtype).astype(np.float64)
    return np.moveaxis((codes * scale).reshape(v.shape), -1, axis)


WIDE = False


def mx_kscale(k):
    if not WIDE:
        return np.ones(k)
    levels = np.array([18, -18])
    if k % 512:
        return np.exp2(np.random.permutation(np.resize(levels, k // 32))).repeat(32)
    a = np.empty((k // 512, 16))
    for p in range(k // 512):
        a[p, :8] = np.random.permutation(np.resize(levels, 8))
        for g in range(8):
            far = levels[np.abs(levels - a[p, g]) >= 10]
            a[p, g + 8] = far[np.random.randint(len(far))]
    return np.exp2(a.ravel()).repeat(32)


BF16 = ml_dtypes.bfloat16


def bf(x):
    return np.asarray(x, np.float32).astype(BF16)


def f64(x):
    return np.asarray(x).astype(np.float64)


B, C, T, E, H = 1, 256, 4, 1024, 8
D = E // H
S = C * T


def join_heads(g):
    return np.moveaxis(g, 1, 3).reshape(B * S, E)


def setup_inputs():
    s = mx_kscale(S)
    uk = mx_kscale(E)
    uv = mx_kscale(E)
    st = s.reshape(1, 1, C, T, 1)
    sc = s.reshape(C, T)[:, 0].reshape(1, 1, C, 1)
    hidden_states = bf(np.random.standard_normal((B, S, E)) * s[None, :, None])
    wk = bf(np.random.standard_normal((E, E)) * 2.0 / np.sqrt(E) / uk[:, None])
    bk = bf(np.random.standard_normal(E) * 0.3)
    wv = bf(np.random.standard_normal((E, E)) * 2.0 / np.sqrt(E) / uv[:, None])
    bv = bf(np.random.standard_normal(E) * 0.3)
    g0 = bf(np.random.standard_normal((B, H, C, T, D)) * np.exp2(np.random.randint(-6, 1, (B, 1, C, T, 1))) / st * uk.reshape(1, H, 1, 1, D))
    g1 = bf(np.random.standard_normal((B, H, C, T, D)) * np.exp2(np.random.randint(-6, 1, (B, 1, C, T, 1))) / st * uv.reshape(1, H, 1, 1, D))
    g2 = bf(np.random.standard_normal((B, H, C, D)) * 2.0 * np.exp2(np.random.randint(-6, 1, (B, 1, C, 1))) / sc * uk.reshape(1, H, 1, D))
    g3 = bf(np.random.standard_normal((B, H, C, D)) * 2.0 * np.exp2(np.random.randint(-6, 1, (B, 1, C, 1))) / sc * uv.reshape(1, H, 1, D))
    return {"hidden_states": hidden_states, "wk": wk, "bk": bk, "wv": wv, "bv": bv,
            "grad_0": g0, "grad_1": g1, "grad_2": g2, "grad_3": g3}


def reference(hidden_states, wk, bk, wv, bv, grad_0, grad_1, grad_2, grad_3):
    dyk = join_heads(f64(grad_0) + f64(grad_2)[:, :, :, None, :] / T)
    dyv = join_heads(f64(grad_1) + f64(grad_3)[:, :, :, None, :] / T)
    dy = np.concatenate([dyk, dyv], axis=1)
    w = np.concatenate([f64(wk), f64(wv)], axis=0)
    dx = mxq(dy, 1, "e5m2") @ mxq(w, 0, "e4m3")
    xq = mxq(f64(hidden_states).reshape(B * S, E), 0, "e4m3")
    dwk = mxq(dyk, 0, "e5m2").T @ xq
    dwv = mxq(dyv, 0, "e5m2").T @ xq
    return dx.reshape(B, S, E), dwk, dwv

@@ -1,0 +1,456 @@
+from contextlib import ExitStack
+
+import concourse.mybir as mybir
+from concourse.masks import make_identity
+
+S, E, H, D, T = 1024, 1024, 8, 128, 4
+FLOPS = 2 * S * E * E * 4
+BYTES = 2 * (3 * S * E + 2 * S * E + 2 * S * E // T) + 4 * 3 * S * E
+
+F32 = mybir.dt.float32
+BF16 = mybir.dt.bfloat16
+U32 = mybir.dt.uint32
+U8 = mybir.dt.uint8
+E4M3 = mybir.dt.float8_e4m3fn_x4
+E5M2 = mybir.dt.float8_e5m2_x4
+
+P = 128
+PACK = 4
+PASS = P * PACK
+N = 512
+RUN = 4
+LOADED, TURNED, RESULTS = 10, 3, 8
+WOVEN = {"vector": 3, "scalar": 2}
+
+
+def tile_chunkedattention_pb_v_kernel(
+    tc, hidden_states, wk, bk, wv, bv, grad_0, grad_1, grad_2, grad_3, out_0, out_1, out_2
+):
+    nc = tc.nc
+    weights = (wk, wv)
+    grads = (grad_0, grad_1)
+    mean_grads = (grad_2, grad_3)
+    weight_grads = (out_1, out_2)
+
+    with ExitStack() as ctx:
+        keep = ctx.enter_context(tc.tile_pool(name="keep", bufs=1))
+        ring = ctx.enter_context(tc.tile_pool(name="ring", bufs=1))
+        psum = ctx.enter_context(tc.psum_pool(name="psum", bufs=1))
+        ctx.enter_context(tc.manual_schedule())
+
+        ident = keep.tile([P, P], F32, name="ident")
+        make_identity(nc, ident[:])
+
+        raw, banks, staged, mx, results = {}, {}, {}, {}, {}
+
+        def bank(index):
+            return psum.tile([P, N], F32, name="bank", tag="bank%d" % index)
+
+        def copy(engine, out, in_):
+            if engine == "vector":
+                nc.vector.tensor_copy(out=out, in_=in_)
+            else:
+                nc.scalar.copy(out=out, in_=in_)
+
+        def load_mean(a, g):
+            tile = keep.tile([P, H, D], BF16, name="mean", tag="mean%d%d" % (a, g))
+            nc.sync.dma_start(out=tile[:], in_=mean_grads[a][0, :, g * P : (g + 1) * P, :].rearrange("h p d -> p h d"))
+            raw["mean", a, g] = tile
+
+        def load_grad(a, g, c):
+            tile = ring.tile([P, 4, T * D], BF16, name="loaded", bufs=LOADED)
+            src = grads[a][0, 4 * c : 4 * c + 4, g * P : (g + 1) * P]
+            nc.sync.dma_start(out=tile[:], in_=src.rearrange("h p t d -> p h (t d)"))
+            raw["grad", a, g, c] = tile
+
+        def load_w(a, c, n):
+            tile = ring.tile([P, PACK, N], BF16, name="loaded", bufs=LOADED)
+            src = weights[a][c * PASS : (c + 1) * PASS, n * N : (n + 1) * N]
+            nc.sync.dma_start(out=tile[:], in_=src.rearrange("(p j) e -> p j e", j=PACK))
+            raw["w", a, c, n] = tile[:]
+
+        def load_x(g):
+            tile = keep.tile([P, PACK, E], BF16, name="x", tag="x%d" % g)
+            src = hidden_states[0, g * PASS : (g + 1) * PASS, :]
+            nc.sync.dma_start(out=tile[:], in_=src.rearrange("(p j) e -> p j e", j=PACK))
+            for n in range(2):
+                raw["x", g, n] = tile[:, :, n * N : (n + 1) * N]
+
+        def scale_mean(a, g):
+            tile = raw["mean", a, g]
+            nc.vector.tensor_scalar(out=tile[:], in0=tile[:], scalar1=1.0 / T, scalar2=None, op0=mybir.AluOpType.mult)
+
+        def add(a, g, c):
+            tile = keep.tile([P, T, PASS], BF16, name="dy", tag="dy%d%d%d" % (a, g, c))
+            nc.vector.tensor_tensor(
+                out=tile[:].rearrange("p t (h d) -> p h t d", d=D),
+                in0=raw["grad", a, g, c][:].rearrange("p h (t d) -> p h t d", d=D),
+                in1=raw["mean", a, g][:, 4 * c : 4 * c + 4, :].unsqueeze(2).to_broadcast([P, 4, T, D]),
+                op=mybir.AluOpType.add,
+            )
+            raw["tok", a, g, c] = tile[:]
+
+        def turn(a, g, c, half, index):
+            words = raw["tok", a, g, c].rearrange("p t f -> p (t f)").bitcast(F32)
+            tile = bank(index)
+            for i in range(4):
+                t, u = 2 * half + i // 2, i % 2
+                nc.tensor.transpose(tile[:, i * P : (i + 1) * P], words[:, 256 * t + u : 256 * (t + 1) : 2], ident[:])
+            banks["turn", a, g, c, half] = tile
+
+        def drain(engine, a, g, c, half):
+            if half == 0:
+                staged["feat", a, g, c] = ring.tile([P, 4 * N], BF16, name="turned", bufs=TURNED, align_bytes=64)
+            words = staged["feat", a, g, c][:].bitcast(F32)
+            copy(
+                engine,
+                words[:, half * N : (half + 1) * N].rearrange("q (t p u) -> q t p u", t=2, u=2),
+                banks["turn", a, g, c, half][:].rearrange("q (t u p) -> q t p u", t=2, u=2),
+            )
+
+        def interleave(engine, dst, src):
+            copy(
+                engine,
+                dst.rearrange("p (c i t) -> p c t i", t=PACK, i=RUN),
+                src.rearrange("p t (c i) -> p c t i", i=RUN),
+            )
+
+        def weave(engine, *key):
+            tile = ring.tile([P, 4 * N], BF16, name="woven", tag="woven" + engine, bufs=WOVEN[engine], align_bytes=64)
+            interleave(engine, tile[:], raw[key])
+            staged[key] = tile
+
+        def quantize(*key):
+            tag = "".join([str(k) for k in key])
+            codes = keep.tile([P, N], U32, name="codes", tag="codes" + tag, align_bytes=64)
+            scales = keep.tile([P, N], U8, name="scales", tag="scales" + tag, align_bytes=64)
+            fmt = E5M2 if key[0] in ("feat", "tok") else E4M3
+            nc.vector.quantize_mx(out=codes[:].bitcast(fmt), scales=scales[:], in_=staged[key][:])
+            mx[key] = (codes, scales)
+
+        def matmul(acc, lhs, column, rhs, start, stop):
+            cols = slice(column, column + P)
+            nc.tensor.matmul_mx(
+                out=acc[:],
+                lhsT=mx[lhs][0][:, cols].bitcast(E5M2),
+                lhsT_scale=mx[lhs][1][:, cols],
+                rhs=mx[rhs][0][:].bitcast(E4M3),
+                rhs_scale=mx[rhs][1][:],
+                start=start,
+                stop=stop,
+            )
+
+        def dx_passes(g, t, n, passes, index=None):
+            if index is not None:
+                banks["dx", g, t, n] = bank(index)
+            for a, c in passes:
+                matmul(banks["dx", g, t, n], ("feat", a, g, c), t * P, ("w", a, c, n), (a, c) == (0, 0), (a, c) == (1, 1))
+
+        def dx_out(engine, g, t, n):
+            if t % 2 == 0:
+                results["dx", g, t // 2, n] = ring.tile([P, E], F32, name="result", bufs=RESULTS)
+            copy(engine, results["dx", g, t // 2, n][:, (t % 2) * N : (t % 2 + 1) * N], banks["dx", g, t, n][:])
+
+        def dx_store(g, pair, n):
+            rows = out_0[0, g * PASS : (g + 1) * PASS, n * N : (n + 1) * N].rearrange("(p t) e -> p t e", t=T)
+            tile = results["dx", g, pair, n]
+            nc.sync.dma_start(out=rows[:, 2 * pair : 2 * pair + 2, :], in_=tile[:].rearrange("p (t e) -> p t e", t=2))
+
+        def dw_group(a, m, n, index):
+            acc = bank(index)
+            for g in range(2):
+                matmul(acc, ("tok", a, g, m // 4), (m % 4) * P, ("x", g, n), g == 0, g == 1)
+            banks["dw", a, m, n] = acc
+
+        def dw_out(engine, a, m, n):
+            if n == 0:
+                results["dw", a, m] = ring.tile([P, E], F32, name="result", bufs=RESULTS)
+            copy(engine, results["dw", a, m][:, n * N : (n + 1) * N], banks["dw", a, m, n][:])
+
+        def dw_store(a, m):
+            nc.sync.dma_start(out=weight_grads[a][m * P : (m + 1) * P, :], in_=results["dw", a, m][:])
+
+        V, A = "vector", "scalar"
+        KEY, VAL = [(0, 0), (0, 1)], [(1, 0), (1, 1)]
+        load_mean(0, 0)
+        load_grad(0, 0, 0)
+        load_w(0, 0, 0)
+        load_grad(0, 0, 1)
+        load_w(0, 1, 0)
+        load_mean(1, 0)
+        load_grad(1, 0, 0)
+        load_w(1, 0, 0)
+        load_grad(1, 0, 1)
+        load_w(1, 1, 0)
+        load_w(0, 0, 1)
+        load_mean(0, 1)
+        load_grad(0, 1, 0)
+        weave(A, "w", 0, 0, 0)
+        scale_mean(0, 0)
+        add(0, 0, 0)
+        load_grad(0, 1, 1)
+        load_mean(1, 1)
+        load_grad(1, 1, 0)
+        turn(0, 0, 0, 0, 0)
+        drain(A, 0, 0, 0, 0)
+        weave(V, "tok", 0, 0, 0)
+        turn(0, 0, 0, 1, 1)
+        drain(A, 0, 0, 0, 1)
+        add(0, 0, 1)
+        load_grad(1, 1, 1)
+        turn(0, 0, 1, 0, 2)
+        drain(A, 0, 0, 1, 0)
+        weave(V, "w", 0, 1, 0)
+        load_w(0, 1, 1)
+        turn(0, 0, 1, 1, 3)
+        drain(A, 0, 0, 1, 1)
+        quantize("w", 0, 0, 0)
+        weave(A, "w", 1, 0, 0)
+        quantize("feat", 0, 0, 0)
+        dx_passes(0, 0, 0, [(0, 0)], 4)
+        scale_mean(1, 0)
+        dx_passes(0, 1, 0, [(0, 0)], 5)
+        add(1, 0, 0)
+        load_w(1, 0, 1)
+        load_w(1, 1, 1)
+        load_x(0)
+        load_x(1)
+        turn(1, 0, 0, 0, 0)
+        drain(A, 1, 0, 0, 0)
+        quantize("w", 0, 1, 0)
+        turn(1, 0, 0, 1, 1)
+        drain(A, 1, 0, 0, 1)
+        quantize("feat", 0, 0, 1)
+        dx_passes(0, 2, 0, [(0, 0)], 6)
+        add(1, 0, 1)
+        dx_passes(0, 3, 0, [(0, 0)], 7)
+        weave(V, "w", 1, 1, 0)
+        dx_passes(0, 0, 0, [(0, 1)])
+        quantize("w", 1, 0, 0)
+        dx_passes(0, 1, 0, [(0, 1)])
+        quantize("feat", 1, 0, 0)
+        turn(1, 0, 1, 0, 2)
+        drain(A, 1, 0, 1, 0)
+        scale_mean(0, 1)
+        turn(1, 0, 1, 1, 3)
+        drain(A, 1, 0, 1, 1)
+        quantize("w", 1, 1, 0)
+        dx_passes(0, 2, 0, [(0, 1)])
+        weave(A, "w", 0, 0, 1)
+        quantize("feat", 1, 0, 1)
+        dx_passes(0, 3, 0, [(0, 1)])
+        add(0, 1, 0)
+        dx_passes(0, 0, 0, [(1, 0)])
+        scale_mean(1, 1)
+        dx_passes(0, 1, 0, [(1, 0)])
+        add(0, 1, 1)
+        dx_passes(0, 2, 0, [(1, 0)])
+        add(1, 1, 0)
+        dx_passes(0, 3, 0, [(1, 0)])
+        add(1, 1, 1)
+        dx_passes(0, 0, 0, [(1, 1)])
+        dx_out(A, 0, 0, 0)
+        quantize("tok", 0, 0, 0)
+        dx_passes(0, 1, 0, [(1, 1)])
+        dx_out(A, 0, 1, 0)
+        dx_store(0, 0, 0)
+        dx_passes(0, 2, 0, [(1, 1)])
+        dx_passes(0, 3, 0, [(1, 1)])
+        turn(0, 1, 0, 0, 0)
+        drain(A, 0, 1, 0, 0)
+        turn(0, 1, 0, 1, 1)
+        drain(A, 0, 1, 0, 1)
+        quantize("feat", 0, 1, 0)
+        turn(0, 1, 1, 0, 2)
+        dx_out(A, 0, 2, 0)
+        quantize("w", 0, 0, 1)
+        turn(0, 1, 1, 1, 3)
+        dx_out(A, 0, 3, 0)
+        dx_store(0, 1, 0)
+        turn(1, 1, 0, 0, 0)
+        drain(A, 0, 1, 1, 0)
+        turn(1, 1, 0, 1, 1)
+        drain(A, 0, 1, 1, 1)
+        quantize("feat", 0, 1, 1)
+        turn(1, 1, 1, 0, 2)
+        drain(A, 1, 1, 0, 0)
+        weave(V, "w", 1, 0, 1)
+        turn(1, 1, 1, 1, 3)
+        drain(A, 1, 1, 0, 1)
+        quantize("feat", 1, 1, 0)
+        dx_passes(1, 0, 0, [(0, 0)], 4)
+        drain(A, 1, 1, 1, 0)
+        dx_passes(1, 1, 0, [(0, 0)], 5)
+        drain(A, 1, 1, 1, 1)
+        quantize("feat", 1, 1, 1)
+        dx_passes(1, 2, 0, [(0, 0)], 6)
+        weave(A, "w", 0, 1, 1)
+        weave(V, "w", 1, 1, 1)
+        dx_passes(1, 3, 0, [(0, 0)], 7)
+        weave(A, "x", 0, 0)
+        quantize("w", 1, 0, 1)
+        dx_passes(1, 0, 0, [(0, 1)])
+        quantize("w", 0, 1, 1)
+        dx_passes(1, 1, 0, [(0, 1)])
+        weave(V, "x", 1, 0)
+        dx_passes(1, 2, 0, [(0, 1)])
+        quantize("w", 1, 1, 1)
+        dx_passes(1, 3, 0, [(0, 1)])
+        weave(V, "x", 1, 1)
+        dx_passes(1, 0, 0, [(1, 0)])
+        quantize("x", 1, 0)
+        dx_passes(1, 1, 0, [(1, 0)])
+        weave(V, "tok", 0, 1, 0)
+        dx_passes(1, 2, 0, [(1, 0)])
+        quantize("x", 1, 1)
+        dx_passes(1, 3, 0, [(1, 0)])
+        quantize("x", 0, 0)
+        dx_passes(1, 0, 0, [(1, 1)])
+        dx_out(A, 1, 0, 0)
+        quantize("tok", 0, 1, 0)
+        dx_passes(1, 1, 0, [(1, 1)])
+        dx_out(A, 1, 1, 0)
+        dx_store(1, 0, 0)
+        dx_passes(1, 2, 0, [(1, 1)])
+        dx_out(A, 1, 2, 0)
+        dx_passes(1, 3, 0, [(1, 1)])
+        dx_out(A, 1, 3, 0)
+        dx_store(1, 1, 0)
+        dx_passes(0, 0, 1, [(0, 0)], 0)
+        weave(A, "x", 0, 1)
+        quantize("x", 0, 1)
+        dx_passes(0, 1, 1, [(0, 0)], 1)
+        weave(V, "tok", 0, 0, 1)
+        dx_passes(0, 2, 1, [(0, 0)], 2)
+        weave(V, "tok", 0, 1, 1)
+        dx_passes(0, 3, 1, [(0, 0)], 3)
+        quantize("tok", 0, 0, 1)
+        dx_passes(0, 0, 1, [(0, 1)])
+        weave(V, "tok", 1, 0, 0)
+        dx_passes(0, 1, 1, [(0, 1)])
+        quantize("tok", 0, 1, 1)
+        dx_passes(0, 2, 1, [(0, 1)])
+        weave(V, "tok", 1, 1, 0)
+        dx_passes(0, 3, 1, [(0, 1)])
+        quantize("tok", 1, 0, 0)
+        dx_passes(0, 0, 1, [(1, 0)])
+        weave(V, "tok", 1, 0, 1)
+        dx_passes(0, 1, 1, [(1, 0)])
+        quantize("tok", 1, 1, 0)
+        dx_passes(0, 2, 1, [(1, 0)])
+        weave(V, "tok", 1, 1, 1)
+        dx_passes(0, 3, 1, [(1, 0)])
+        quantize("tok", 1, 0, 1)
+        dx_passes(0, 0, 1, [(1, 1)])
+        dx_out(A, 0, 0, 1)
+        quantize("tok", 1, 1, 1)
+        dx_passes(0, 1, 1, [(1, 1)])
+        dx_out(A, 0, 1, 1)
+        dx_store(0, 0, 1)
+        dx_passes(0, 2, 1, [(1, 1)])
+        dx_out(A, 0, 2, 1)
+        dx_passes(0, 3, 1, [(1, 1)])
+        dx_out(A, 0, 3, 1)
+        dx_store(0, 1, 1)
+        dx_passes(1, 0, 1, [(0, 0)], 4)
+        dx_passes(1, 0, 1, [(0, 1)])
+        dx_passes(1, 0, 1, [(1, 0)])
+        dx_passes(1, 0, 1, [(1, 1)])
+        dx_out(A, 1, 0, 1)
+        dx_passes(1, 1, 1, [(0, 0)], 5)
+        dx_passes(1, 1, 1, [(0, 1)])
+        dx_passes(1, 1, 1, [(1, 0)])
+        dx_passes(1, 1, 1, [(1, 1)])
+        dx_out(A, 1, 1, 1)
+        dx_store(1, 0, 1)
+        dx_passes(1, 2, 1, [(0, 0)], 6)
+        dx_passes(1, 2, 1, [(0, 1)])
+        dx_passes(1, 2, 1, [(1, 0)])
+        dx_passes(1, 2, 1, [(1, 1)])
+        dx_out(A, 1, 2, 1)
+        dx_passes(1, 3, 1, [(0, 0)], 7)
+        dx_passes(1, 3, 1, [(0, 1)])
+        dx_passes(1, 3, 1, [(1, 0)])
+        dx_passes(1, 3, 1, [(1, 1)])
+        dx_out(A, 1, 3, 1)
+        dx_store(1, 1, 1)
+        dw_group(0, 0, 0, 0)
+        dw_out(A, 0, 0, 0)
+        dw_group(0, 0, 1, 1)
+        dw_out(A, 0, 0, 1)
+        dw_store(0, 0)
+        dw_group(0, 1, 0, 2)
+        dw_out(A, 0, 1, 0)
+        dw_group(0, 1, 1, 3)
+        dw_out(A, 0, 1, 1)
+        dw_store(0, 1)
+        dw_group(0, 2, 0, 4)
+        dw_out(A, 0, 2, 0)
+        dw_group(0, 2, 1, 5)
+        dw_out(A, 0, 2, 1)
+        dw_store(0, 2)
+        dw_group(0, 3, 0, 6)
+        dw_out(A, 0, 3, 0)
+        dw_group(0, 3, 1, 7)
+        dw_out(A, 0, 3, 1)
+        dw_store(0, 3)
+        dw_group(0, 4, 0, 0)
+        dw_out(A, 0, 4, 0)
+        dw_group(0, 4, 1, 1)
+        dw_out(A, 0, 4, 1)
+        dw_store(0, 4)
+        dw_group(0, 5, 0, 2)
+        dw_out(A, 0, 5, 0)
+        dw_group(0, 5, 1, 3)
+        dw_out(A, 0, 5, 1)
+        dw_store(0, 5)
+        dw_group(0, 6, 0, 4)
+        dw_out(A, 0, 6, 0)
+        dw_group(0, 6, 1, 5)
+        dw_out(A, 0, 6, 1)
+        dw_store(0, 6)
+        dw_group(0, 7, 0, 6)
+        dw_out(A, 0, 7, 0)
+        dw_group(0, 7, 1, 7)
+        dw_out(A, 0, 7, 1)
+        dw_store(0, 7)
+        dw_group(1, 0, 0, 0)
+        dw_out(A, 1, 0, 0)
+        dw_group(1, 0, 1, 1)
+        dw_out(V, 1, 0, 1)
+        dw_store(1, 0)
+        dw_group(1, 1, 0, 2)
+        dw_out(A, 1, 1, 0)
+        dw_group(1, 1, 1, 3)
+        dw_out(V, 1, 1, 1)
+        dw_store(1, 1)
+        dw_group(1, 2, 0, 4)
+        dw_out(A, 1, 2, 0)
+        dw_group(1, 2, 1, 5)
+        dw_out(V, 1, 2, 1)
+        dw_store(1, 2)
+        dw_group(1, 3, 0, 6)
+        dw_out(A, 1, 3, 0)
+        dw_group(1, 3, 1, 7)
+        dw_out(V, 1, 3, 1)
+        dw_store(1, 3)
+        dw_group(1, 4, 0, 0)
+        dw_out(A, 1, 4, 0)
+        dw_group(1, 4, 1, 1)
+        dw_out(V, 1, 4, 1)
+        dw_store(1, 4)
+        dw_group(1, 5, 0, 2)
+        dw_out(A, 1, 5, 0)
+        dw_group(1, 5, 1, 3)
+        dw_out(V, 1, 5, 1)
+        dw_store(1, 5)
+        dw_group(1, 6, 0, 4)
+        dw_out(A, 1, 6, 0)
+        dw_group(1, 6, 1, 5)
+        dw_out(V, 1, 6, 1)
+        dw_store(1, 6)
+        dw_group(1, 7, 0, 6)
+        dw_out(A, 1, 7, 0)
+        dw_group(1, 7, 1, 7)
+        dw_out(V, 1, 7, 1)
+        dw_store(1, 7)

@@ -19,8 +19,9 @@ PACK = 4
 PASS = P * PACK
 N = 512
 RUN = 4
-LOADED, TURNED, RESULTS = 10, 3, 8
-WOVEN = {"vector": 3, "scalar": 2}
+LOADED, WIDE, TURNED, RESULTS = 6, 4, 3, 8
+WOVEN = {"vector": 4, "scalar": 2}
+CODES = {"w": 8, "x": 4, "feat": 8, "tok": 5}
 
 
 def tile_chunkedattention_pb_v_kernel(
@@ -63,18 +64,17 @@ def tile_chunkedattention_pb_v_kernel(
             nc.sync.dma_start(out=tile[:], in_=src.rearrange("h p t d -> p h (t d)"))
             raw["grad", a, g, c] = tile
 
-        def load_w(a, c, n):
-            tile = ring.tile([P, PACK, N], BF16, name="loaded", bufs=LOADED)
-            src = weights[a][c * PASS : (c + 1) * PASS, n * N : (n + 1) * N]
-            nc.sync.dma_start(out=tile[:], in_=src.rearrange("(p j) e -> p j e", j=PACK))
-            raw["w", a, c, n] = tile[:]
-
-        def load_x(g):
-            tile = keep.tile([P, PACK, E], BF16, name="x", tag="x%d" % g)
-            src = hidden_states[0, g * PASS : (g + 1) * PASS, :]
+        def load_wide(key, src):
+            tile = ring.tile([P, PACK, E], BF16, name="wide", bufs=WIDE)
             nc.sync.dma_start(out=tile[:], in_=src.rearrange("(p j) e -> p j e", j=PACK))
             for n in range(2):
-                raw["x", g, n] = tile[:, :, n * N : (n + 1) * N]
+                raw[key + (n,)] = tile[:, :, n * N : (n + 1) * N]
+
+        def load_w(a, c):
+            load_wide(("w", a, c), weights[a][c * PASS : (c + 1) * PASS, :])
+
+        def load_x(g):
+            load_wide(("x", g), hidden_states[0, g * PASS : (g + 1) * PASS, :])
 
         def scale_mean(a, g):
             tile = raw["mean", a, g]
@@ -121,9 +121,9 @@ def tile_chunkedattention_pb_v_kernel(
             staged[key] = tile
 
         def quantize(*key):
-            tag = "".join([str(k) for k in key])
-            codes = keep.tile([P, N], U32, name="codes", tag="codes" + tag, align_bytes=64)
-            scales = keep.tile([P, N], U8, name="scales", tag="scales" + tag, align_bytes=64)
+            kind = key[0]
+            codes = ring.tile([P, N], U32, name="codes", tag="codes_" + kind, bufs=CODES[kind], align_bytes=64)
+            scales = ring.tile([P, N], U8, name="scales", tag="scales_" + kind, bufs=CODES[kind], align_bytes=64)
             fmt = E5M2 if key[0] in ("feat", "tok") else E4M3
             nc.vector.quantize_mx(out=codes[:].bitcast(fmt), scales=scales[:], in_=staged[key][:])
             mx[key] = (codes, scales)
@@ -147,14 +147,13 @@ def tile_chunkedattention_pb_v_kernel(
                 matmul(banks["dx", g, t, n], ("feat", a, g, c), t * P, ("w", a, c, n), (a, c) == (0, 0), (a, c) == (1, 1))
 
         def dx_out(engine, g, t, n):
-            if t % 2 == 0:
-                results["dx", g, t // 2, n] = ring.tile([P, E], F32, name="result", bufs=RESULTS)
-            copy(engine, results["dx", g, t // 2, n][:, (t % 2) * N : (t % 2 + 1) * N], banks["dx", g, t, n][:])
+            if n == 0:
+                results["dx", g, t] = ring.tile([P, E], F32, name="result", bufs=RESULTS)
+            copy(engine, results["dx", g, t][:, n * N : (n + 1) * N], banks["dx", g, t, n][:])
 
-        def dx_store(g, pair, n):
-            rows = out_0[0, g * PASS : (g + 1) * PASS, n * N : (n + 1) * N].rearrange("(p t) e -> p t e", t=T)
-            tile = results["dx", g, pair, n]
-            nc.sync.dma_start(out=rows[:, 2 * pair : 2 * pair + 2, :], in_=tile[:].rearrange("p (t e) -> p t e", t=2))
+        def dx_store(g, t):
+            rows = out_0[0, g * PASS : (g + 1) * PASS, :].rearrange("(p t) e -> t p e", t=T)
+            nc.sync.dma_start(out=rows[t], in_=results["dx", g, t][:])
 
         def dw_group(a, m, n, index):
             acc = bank(index)
@@ -174,86 +173,91 @@ def tile_chunkedattention_pb_v_kernel(
         KEY, VAL = [(0, 0), (0, 1)], [(1, 0), (1, 1)]
         load_mean(0, 0)
         load_grad(0, 0, 0)
-        load_w(0, 0, 0)
+        load_w(0, 0)
         load_grad(0, 0, 1)
-        load_w(0, 1, 0)
+        load_w(0, 1)
         load_mean(1, 0)
         load_grad(1, 0, 0)
-        load_w(1, 0, 0)
+        load_w(1, 0)
         load_grad(1, 0, 1)
-        load_w(1, 1, 0)
-        load_w(0, 0, 1)
+        load_w(1, 1)
         load_mean(0, 1)
         load_grad(0, 1, 0)
-        weave(A, "w", 0, 0, 0)
-        scale_mean(0, 0)
-        add(0, 0, 0)
         load_grad(0, 1, 1)
         load_mean(1, 1)
+        scale_mean(0, 0)
+        add(0, 0, 0)
         load_grad(1, 1, 0)
         turn(0, 0, 0, 0, 0)
         drain(A, 0, 0, 0, 0)
-        weave(V, "tok", 0, 0, 0)
+        weave(V, "w", 0, 0, 0)
         turn(0, 0, 0, 1, 1)
         drain(A, 0, 0, 0, 1)
         add(0, 0, 1)
         load_grad(1, 1, 1)
         turn(0, 0, 1, 0, 2)
-        drain(A, 0, 0, 1, 0)
-        weave(V, "w", 0, 1, 0)
-        load_w(0, 1, 1)
-        turn(0, 0, 1, 1, 3)
-        drain(A, 0, 0, 1, 1)
+        weave(A, "w", 0, 0, 1)
         quantize("w", 0, 0, 0)
-        weave(A, "w", 1, 0, 0)
+        load_x(0)
+        turn(0, 0, 1, 1, 3)
+        drain(A, 0, 0, 1, 0)
         quantize("feat", 0, 0, 0)
         dx_passes(0, 0, 0, [(0, 0)], 4)
-        scale_mean(1, 0)
+        drain(A, 0, 0, 1, 1)
+        weave(V, "w", 0, 1, 0)
         dx_passes(0, 1, 0, [(0, 0)], 5)
-        add(1, 0, 0)
-        load_w(1, 0, 1)
-        load_w(1, 1, 1)
-        load_x(0)
+        weave(A, "w", 0, 1, 1)
+        scale_mean(1, 0)
         load_x(1)
+        dx_passes(0, 2, 0, [(0, 0)], 6)
+        quantize("w", 0, 0, 1)
+        dx_passes(0, 3, 0, [(0, 0)], 7)
+        add(1, 0, 0)
         turn(1, 0, 0, 0, 0)
         drain(A, 1, 0, 0, 0)
         quantize("w", 0, 1, 0)
         turn(1, 0, 0, 1, 1)
         drain(A, 1, 0, 0, 1)
         quantize("feat", 0, 0, 1)
-        dx_passes(0, 2, 0, [(0, 0)], 6)
+        dx_passes(0, 0, 1, [(0, 0)], 2)
+        weave(A, "w", 1, 0, 1)
+        weave(V, "w", 1, 0, 0)
+        dx_passes(0, 1, 1, [(0, 0)], 3)
         add(1, 0, 1)
-        dx_passes(0, 3, 0, [(0, 0)], 7)
-        weave(V, "w", 1, 1, 0)
         dx_passes(0, 0, 0, [(0, 1)])
-        quantize("w", 1, 0, 0)
+        quantize("w", 0, 1, 1)
         dx_passes(0, 1, 0, [(0, 1)])
-        quantize("feat", 1, 0, 0)
-        turn(1, 0, 1, 0, 2)
-        drain(A, 1, 0, 1, 0)
-        scale_mean(0, 1)
-        turn(1, 0, 1, 1, 3)
-        drain(A, 1, 0, 1, 1)
-        quantize("w", 1, 1, 0)
+        quantize("w", 1, 0, 0)
         dx_passes(0, 2, 0, [(0, 1)])
-        weave(A, "w", 0, 0, 1)
-        quantize("feat", 1, 0, 1)
+        quantize("feat", 1, 0, 0)
         dx_passes(0, 3, 0, [(0, 1)])
-        add(0, 1, 0)
+        weave(V, "w", 1, 1, 0)
+        dx_passes(0, 0, 1, [(0, 1)])
+        quantize("w", 1, 0, 1)
+        dx_passes(0, 1, 1, [(0, 1)])
+        turn(1, 0, 1, 0, 0)
+        drain(A, 1, 0, 1, 0)
+        turn(1, 0, 1, 1, 1)
+        drain(A, 1, 0, 1, 1)
+        quantize("feat", 1, 0, 1)
         dx_passes(0, 0, 0, [(1, 0)])
-        scale_mean(1, 1)
+        weave(A, "w", 1, 1, 1)
+        quantize("w", 1, 1, 0)
         dx_passes(0, 1, 0, [(1, 0)])
-        add(0, 1, 1)
+        scale_mean(0, 1)
         dx_passes(0, 2, 0, [(1, 0)])
-        add(1, 1, 0)
+        add(0, 1, 0)
         dx_passes(0, 3, 0, [(1, 0)])
-        add(1, 1, 1)
+        quantize("w", 1, 1, 1)
+        dx_passes(0, 0, 1, [(1, 0)])
+        add(0, 1, 1)
+        dx_passes(0, 1, 1, [(1, 0)])
+        scale_mean(1, 1)
         dx_passes(0, 0, 0, [(1, 1)])
         dx_out(A, 0, 0, 0)
-        quantize("tok", 0, 0, 0)
+        add(1, 1, 0)
         dx_passes(0, 1, 0, [(1, 1)])
         dx_out(A, 0, 1, 0)
-        dx_store(0, 0, 0)
         dx_passes(0, 2, 0, [(1, 1)])
         dx_passes(0, 3, 0, [(1, 1)])
         turn(0, 1, 0, 0, 0)
@@ -261,196 +265,187 @@ def tile_chunkedattention_pb_v_kernel(
         turn(0, 1, 0, 1, 1)
         drain(A, 0, 1, 0, 1)
         quantize("feat", 0, 1, 0)
-        turn(0, 1, 1, 0, 2)
+        dx_passes(0, 0, 1, [(1, 1)])
         dx_out(A, 0, 2, 0)
-        quantize("w", 0, 0, 1)
-        turn(0, 1, 1, 1, 3)
+        add(1, 1, 1)
+        dx_passes(0, 1, 1, [(1, 1)])
         dx_out(A, 0, 3, 0)
-        dx_store(0, 1, 0)
-        turn(1, 1, 0, 0, 0)
+        weave(V, "x", 0, 0)
+        dx_passes(0, 2, 1, [(0, 0)], 4)
+        dx_out(A, 0, 0, 1)
+        dx_store(0, 0)
+        dx_passes(0, 2, 1, [(0, 1)])
+        dx_out(A, 0, 1, 1)
+        dx_store(0, 1)
+        dx_passes(0, 2, 1, [(1, 0)])
+        dx_passes(0, 2, 1, [(1, 1)])
+        turn(0, 1, 1, 0, 0)
         drain(A, 0, 1, 1, 0)
-        turn(1, 1, 0, 1, 1)
+        turn(0, 1, 1, 1, 1)
         drain(A, 0, 1, 1, 1)
         quantize("feat", 0, 1, 1)
-        turn(1, 1, 1, 0, 2)
-        drain(A, 1, 1, 0, 0)
-        weave(V, "w", 1, 0, 1)
-        turn(1, 1, 1, 1, 3)
-        drain(A, 1, 1, 0, 1)
-        quantize("feat", 1, 1, 0)
-        dx_passes(1, 0, 0, [(0, 0)], 4)
-        drain(A, 1, 1, 1, 0)
-        dx_passes(1, 1, 0, [(0, 0)], 5)
-        drain(A, 1, 1, 1, 1)
-        quantize("feat", 1, 1, 1)
-        dx_passes(1, 2, 0, [(0, 0)], 6)
-        weave(A, "w", 0, 1, 1)
-        weave(V, "w", 1, 1, 1)
-        dx_passes(1, 3, 0, [(0, 0)], 7)
-        weave(A, "x", 0, 0)
-        quantize("w", 1, 0, 1)
-        dx_passes(1, 0, 0, [(0, 1)])
-        quantize("w", 0, 1, 1)
-        dx_passes(1, 1, 0, [(0, 1)])
-        weave(V, "x", 1, 0)
-        dx_passes(1, 2, 0, [(0, 1)])
-        quantize("w", 1, 1, 1)
-        dx_passes(1, 3, 0, [(0, 1)])
-        weave(V, "x", 1, 1)
-        dx_passes(1, 0, 0, [(1, 0)])
-        quantize("x", 1, 0)
-        dx_passes(1, 1, 0, [(1, 0)])
-        weave(V, "tok", 0, 1, 0)
-        dx_passes(1, 2, 0, [(1, 0)])
-        quantize("x", 1, 1)
-        dx_passes(1, 3, 0, [(1, 0)])
-        quantize("x", 0, 0)
-        dx_passes(1, 0, 0, [(1, 1)])
-        dx_out(A, 1, 0, 0)
-        quantize("tok", 0, 1, 0)
-        dx_passes(1, 1, 0, [(1, 1)])
-        dx_out(A, 1, 1, 0)
-        dx_store(1, 0, 0)
-        dx_passes(1, 2, 0, [(1, 1)])
-        dx_out(A, 1, 2, 0)
-        dx_passes(1, 3, 0, [(1, 1)])
-        dx_out(A, 1, 3, 0)
-        dx_store(1, 1, 0)
-        dx_passes(0, 0, 1, [(0, 0)], 0)
-        weave(A, "x", 0, 1)
-        quantize("x", 0, 1)
-        dx_passes(0, 1, 1, [(0, 0)], 1)
-        weave(V, "tok", 0, 0, 1)
-        dx_passes(0, 2, 1, [(0, 0)], 2)
-        weave(V, "tok", 0, 1, 1)
-        dx_passes(0, 3, 1, [(0, 0)], 3)
-        quantize("tok", 0, 0, 1)
-        dx_passes(0, 0, 1, [(0, 1)])
-        weave(V, "tok", 1, 0, 0)
-        dx_passes(0, 1, 1, [(0, 1)])
-        quantize("tok", 0, 1, 1)
-        dx_passes(0, 2, 1, [(0, 1)])
-        weave(V, "tok", 1, 1, 0)
-        dx_passes(0, 3, 1, [(0, 1)])
-        quantize("tok", 1, 0, 0)
-        dx_passes(0, 0, 1, [(1, 0)])
-        weave(V, "tok", 1, 0, 1)
-        dx_passes(0, 1, 1, [(1, 0)])
-        quantize("tok", 1, 1, 0)
-        dx_passes(0, 2, 1, [(1, 0)])
-        weave(V, "tok", 1, 1, 1)
-        dx_passes(0, 3, 1, [(1, 0)])
-        quantize("tok", 1, 0, 1)
-        dx_passes(0, 0, 1, [(1, 1)])
-        dx_out(A, 0, 0, 1)
-        quantize("tok", 1, 1, 1)
-        dx_passes(0, 1, 1, [(1, 1)])
-        dx_out(A, 0, 1, 1)
-        dx_store(0, 0, 1)
-        dx_passes(0, 2, 1, [(1, 1)])
+        dx_passes(0, 3, 1, [(0, 0)], 5)
         dx_out(A, 0, 2, 1)
+        weave(V, "tok", 0, 0, 0)
+        dx_store(0, 2)
+        dx_passes(0, 3, 1, [(0, 1)])
+        dx_passes(0, 3, 1, [(1, 0)])
         dx_passes(0, 3, 1, [(1, 1)])
         dx_out(A, 0, 3, 1)
-        dx_store(0, 1, 1)
-        dx_passes(1, 0, 1, [(0, 0)], 4)
+        dx_store(0, 3)
+        turn(1, 1, 0, 0, 6)
+        drain(A, 1, 1, 0, 0)
+        turn(1, 1, 0, 1, 7)
+        drain(A, 1, 1, 0, 1)
+        quantize("feat", 1, 1, 0)
+        dx_passes(1, 0, 0, [(0, 0)], 2)
+        weave(V, "tok", 0, 1, 0)
+        dx_passes(1, 0, 1, [(0, 0)], 3)
+        turn(1, 1, 1, 0, 0)
+        drain(A, 1, 1, 1, 0)
+        turn(1, 1, 1, 1, 1)
+        drain(A, 1, 1, 1, 1)
+        quantize("feat", 1, 1, 1)
+        dx_passes(1, 1, 0, [(0, 0)], 4)
+        weave(A, "x", 0, 1)
+        quantize("tok", 0, 0, 0)
+        dx_passes(1, 1, 1, [(0, 0)], 5)
+        weave(V, "x", 1, 0)
+        dx_passes(1, 0, 0, [(0, 1)])
+        quantize("x", 0, 0)
         dx_passes(1, 0, 1, [(0, 1)])
+        weave(V, "x", 1, 1)
+        dx_passes(1, 1, 0, [(0, 1)])
+        quantize("tok", 0, 1, 0)
+        dx_passes(1, 1, 1, [(0, 1)])
+        quantize("x", 1, 0)
+        dx_passes(1, 2, 0, [(0, 0)], 6)
+        quantize("x", 0, 1)
+        dx_passes(1, 2, 1, [(0, 0)], 7)
+        quantize("x", 1, 1)
+        dx_passes(1, 0, 0, [(1, 0)])
+        weave(V, "tok", 0, 0, 1)
+        dx_passes(1, 0, 0, [(1, 1)])
+        dx_out(A, 1, 0, 0)
+        weave(V, "tok", 0, 1, 1)
         dx_passes(1, 0, 1, [(1, 0)])
+        quantize("tok", 0, 0, 1)
         dx_passes(1, 0, 1, [(1, 1)])
         dx_out(A, 1, 0, 1)
-        dx_passes(1, 1, 1, [(0, 0)], 5)
-        dx_passes(1, 1, 1, [(0, 1)])
+        weave(V, "tok", 1, 0, 0)
+        dx_store(1, 0)
+        dx_passes(1, 1, 0, [(1, 0)])
+        quantize("tok", 0, 1, 1)
+        dx_passes(1, 1, 0, [(1, 1)])
+        dx_out(A, 1, 1, 0)
+        weave(V, "tok", 1, 1, 0)
         dx_passes(1, 1, 1, [(1, 0)])
+        quantize("tok", 1, 0, 0)
         dx_passes(1, 1, 1, [(1, 1)])
         dx_out(A, 1, 1, 1)
-        dx_store(1, 0, 1)
-        dx_passes(1, 2, 1, [(0, 0)], 6)
+        weave(V, "tok", 1, 0, 1)
+        dx_store(1, 1)
+        dx_passes(1, 2, 0, [(0, 1)])
+        dx_passes(1, 2, 0, [(1, 0)])
+        dx_passes(1, 2, 0, [(1, 1)])
+        dx_out(A, 1, 2, 0)
         dx_passes(1, 2, 1, [(0, 1)])
         dx_passes(1, 2, 1, [(1, 0)])
         dx_passes(1, 2, 1, [(1, 1)])
         dx_out(A, 1, 2, 1)
-        dx_passes(1, 3, 1, [(0, 0)], 7)
+        dx_store(1, 2)
+        dx_passes(1, 3, 0, [(0, 0)], 0)
+        dx_passes(1, 3, 0, [(0, 1)])
+        dx_passes(1, 3, 0, [(1, 0)])
+        dx_passes(1, 3, 0, [(1, 1)])
+        dx_out(A, 1, 3, 0)
+        dx_passes(1, 3, 1, [(0, 0)], 1)
         dx_passes(1, 3, 1, [(0, 1)])
         dx_passes(1, 3, 1, [(1, 0)])
         dx_passes(1, 3, 1, [(1, 1)])
         dx_out(A, 1, 3, 1)
-        dx_store(1, 1, 1)
-        dw_group(0, 0, 0, 0)
+        dx_store(1, 3)
+        dw_group(0, 0, 0, 2)
         dw_out(A, 0, 0, 0)
-        dw_group(0, 0, 1, 1)
+        dw_group(0, 0, 1, 3)
         dw_out(A, 0, 0, 1)
         dw_store(0, 0)
-        dw_group(0, 1, 0, 2)
+        dw_group(0, 1, 0, 4)
         dw_out(A, 0, 1, 0)
-        dw_group(0, 1, 1, 3)
+        dw_group(0, 1, 1, 5)
         dw_out(A, 0, 1, 1)
         dw_store(0, 1)
-        dw_group(0, 2, 0, 4)
+        dw_group(0, 2, 0, 6)
         dw_out(A, 0, 2, 0)
-        dw_group(0, 2, 1, 5)
+        dw_group(0, 2, 1, 7)
         dw_out(A, 0, 2, 1)
         dw_store(0, 2)
-        dw_group(0, 3, 0, 6)
+        dw_group(0, 3, 0, 0)
         dw_out(A, 0, 3, 0)
-        dw_group(0, 3, 1, 7)
+        dw_group(0, 3, 1, 1)
         dw_out(A, 0, 3, 1)
+        quantize("tok", 1, 1, 0)
         dw_store(0, 3)
-        dw_group(0, 4, 0, 0)
+        dw_group(0, 4, 0, 2)
         dw_out(A, 0, 4, 0)
-        dw_group(0, 4, 1, 1)
+        weave(V, "tok", 1, 1, 1)
+        dw_group(0, 4, 1, 3)
         dw_out(A, 0, 4, 1)
+        quantize("tok", 1, 0, 1)
         dw_store(0, 4)
-        dw_group(0, 5, 0, 2)
+        dw_group(0, 5, 0, 4)
         dw_out(A, 0, 5, 0)
-        dw_group(0, 5, 1, 3)
+        dw_group(0, 5, 1, 5)
         dw_out(A, 0, 5, 1)
         dw_store(0, 5)
-        dw_group(0, 6, 0, 4)
+        dw_group(0, 6, 0, 6)
         dw_out(A, 0, 6, 0)
-        dw_group(0, 6, 1, 5)
+        dw_group(0, 6, 1, 7)
         dw_out(A, 0, 6, 1)
         dw_store(0, 6)
-        dw_group(0, 7, 0, 6)
+        dw_group(0, 7, 0, 0)
         dw_out(A, 0, 7, 0)
-        dw_group(0, 7, 1, 7)
+        dw_group(0, 7, 1, 1)
         dw_out(A, 0, 7, 1)
+        quantize("tok", 1, 1, 1)
         dw_store(0, 7)
-        dw_group(1, 0, 0, 0)
+        dw_group(1, 0, 0, 2)
         dw_out(A, 1, 0, 0)
-        dw_group(1, 0, 1, 1)
-        dw_out(V, 1, 0, 1)
+        dw_group(1, 0, 1, 3)
+        dw_out(A, 1, 0, 1)
         dw_store(1, 0)
-        dw_group(1, 1, 0, 2)
+        dw_group(1, 1, 0, 4)
         dw_out(A, 1, 1, 0)
-        dw_group(1, 1, 1, 3)
+        dw_group(1, 1, 1, 5)
         dw_out(V, 1, 1, 1)
         dw_store(1, 1)
-        dw_group(1, 2, 0, 4)
+        dw_group(1, 2, 0, 6)
         dw_out(A, 1, 2, 0)
-        dw_group(1, 2, 1, 5)
+        dw_group(1, 2, 1, 7)
         dw_out(V, 1, 2, 1)
         dw_store(1, 2)
-        dw_group(1, 3, 0, 6)
+        dw_group(1, 3, 0, 0)
         dw_out(A, 1, 3, 0)
-        dw_group(1, 3, 1, 7)
+        dw_group(1, 3, 1, 1)
         dw_out(V, 1, 3, 1)
         dw_store(1, 3)
-        dw_group(1, 4, 0, 0)
+        dw_group(1, 4, 0, 2)
         dw_out(A, 1, 4, 0)
-        dw_group(1, 4, 1, 1)
+        dw_group(1, 4, 1, 3)
         dw_out(V, 1, 4, 1)
         dw_store(1, 4)
-        dw_group(1, 5, 0, 2)
+        dw_group(1, 5, 0, 4)
         dw_out(A, 1, 5, 0)
-        dw_group(1, 5, 1, 3)
+        dw_group(1, 5, 1, 5)
         dw_out(V, 1, 5, 1)
         dw_store(1, 5)
-        dw_group(1, 6, 0, 4)
+        dw_group(1, 6, 0, 6)
         dw_out(A, 1, 6, 0)
-        dw_group(1, 6, 1, 5)
+        dw_group(1, 6, 1, 7)
         dw_out(V, 1, 6, 1)
         dw_store(1, 6)
-        dw_group(1, 7, 0, 6)
+        dw_group(1, 7, 0, 0)
         dw_out(A, 1, 7, 0)
-        dw_group(1, 7, 1, 7)
+        dw_group(1, 7, 1, 1)
         dw_out(V, 1, 7, 1)
         dw_store(1, 7)

@@ -54,7 +54,7 @@ def tile_chunkedattention_pb_v_kernel(
                 nc.scalar.copy(out=out, in_=in_)
 
         def load_mean(a, g):
-            tile = keep.tile([P, H, D], BF16, name="mean", tag="mean%d%d" % (a, g))
+            tile = ring.tile([P, H, D], BF16, name="mean", bufs=2)
             nc.sync.dma_start(out=tile[:], in_=mean_grads[a][0, :, g * P : (g + 1) * P, :].rearrange("h p d -> p h d"))
             raw["mean", a, g] = tile
 
@@ -77,25 +77,36 @@ def tile_chunkedattention_pb_v_kernel(
             load_wide(("x", g), hidden_states[0, g * PASS : (g + 1) * PASS, :])
 
         def scale_mean(a, g):
-            tile = raw["mean", a, g]
-            nc.vector.tensor_scalar(out=tile[:], in0=tile[:], scalar1=1.0 / T, scalar2=None, op0=mybir.AluOpType.mult)
+            tile = keep.tile([P, E], BF16, name="share", tag="share%d%d" % (a, g))
+            nc.vector.tensor_scalar(
+                out=tile[:].rearrange("p (u w e) -> p u w e", u=2, e=2),
+                in0=raw["mean", a, g][:].rearrange("p h (w u e) -> p u (h w) e", u=2, e=2),
+                scalar1=1.0 / T,
+                scalar2=None,
+                op0=mybir.AluOpType.mult,
+            )
+            raw["share", a, g] = tile
 
         def add(a, g, c):
-            tile = keep.tile([P, T, PASS], BF16, name="dy", tag="dy%d%d%d" % (a, g, c))
-            nc.vector.tensor_tensor(
-                out=tile[:].rearrange("p t (h d) -> p h t d", d=D),
-                in0=raw["grad", a, g, c][:].rearrange("p h (t d) -> p h t d", d=D),
-                in1=raw["mean", a, g][:, 4 * c : 4 * c + 4, :].unsqueeze(2).to_broadcast([P, 4, T, D]),
-                op=mybir.AluOpType.add,
-            )
+            tile = keep.tile([P, T * PASS], BF16, name="dy", tag="dy%d%d%d" % (a, g, c))
+            out = tile[:].rearrange("p (u t h w e) -> p u h t w e", u=2, t=T, h=4, e=2)
+            grad = raw["grad", a, g, c][:].rearrange("p h (t w u e) -> p u h t w e", t=T, u=2, e=2)
+            share = raw["share", a, g][:].rearrange("p (u h w e) -> p u h w e", u=2, h=H, e=2)
+            for u in range(2):
+                nc.vector.tensor_tensor(
+                    out=out[:, u],
+                    in0=grad[:, u],
+                    in1=share[:, u, 4 * c : 4 * c + 4].unsqueeze(2).to_broadcast([P, 4, T, 32, 2]),
+                    op=mybir.AluOpType.add,
+                )
             raw["tok", a, g, c] = tile[:]
 
         def turn(a, g, c, half, index):
-            words = raw["tok", a, g, c].rearrange("p t f -> p (t f)").bitcast(F32)
+            words = raw["tok", a, g, c].bitcast(F32)
             tile = bank(index)
             for i in range(4):
-                t, u = 2 * half + i // 2, i % 2
-                nc.tensor.transpose(tile[:, i * P : (i + 1) * P], words[:, 256 * t + u : 256 * (t + 1) : 2], ident[:])
+                block = T * (i % 2) + 2 * half + i // 2
+                nc.tensor.transpose(tile[:, i * P : (i + 1) * P], words[:, block * P : (block + 1) * P], ident[:])
             banks["turn", a, g, c, half] = tile
 
         def drain(engine, a, g, c, half):
@@ -115,10 +126,19 @@ def tile_chunkedattention_pb_v_kernel(
                 src.rearrange("p t (c i) -> p c t i", i=RUN),
             )
 
-        def weave(engine, *key):
-            tile = ring.tile([P, 4 * N], BF16, name="woven", tag="woven" + engine, bufs=WOVEN[engine], align_bytes=64)
-            interleave(engine, tile[:], raw[key])
-            staged[key] = tile
+        def weave(engine, *key, halves=(0, 1)):
+            if halves[0] == 0:
+                staged[key] = ring.tile([P, 4 * N], BF16, name="woven", tag="woven" + engine, bufs=WOVEN[engine], align_bytes=64)
+            tile = staged[key]
+            lo, hi = halves[0], halves[-1] + 1
+            if key[0] == "tok":
+                copy(
+                    engine,
+                    tile[:].rearrange("p (u e w t) -> p u w t e", u=2, e=2, t=PACK)[:, lo:hi],
+                    raw[key].rearrange("p (u t w e) -> p u w t e", u=2, t=PACK, e=2)[:, lo:hi],
+                )
+            else:
+                interleave(engine, tile[:, lo * 2 * N : hi * 2 * N], raw[key][:, :, lo * 256 : hi * 256])
 
         def quantize(*key):
             kind = key[0]
@@ -166,14 +186,15 @@ def tile_chunkedattention_pb_v_kernel(
                 results["dw", a, m] = ring.tile([P, E], F32, name="result", bufs=RESULTS)
             copy(engine, results["dw", a, m][:, n * N : (n + 1) * N], banks["dw", a, m, n][:])
 
-        def dw_store(a, m):
-            nc.sync.dma_start(out=weight_grads[a][m * P : (m + 1) * P, :], in_=results["dw", a, m][:])
+        def dw_store(a, m, cols=slice(0, E)):
+            rows = weight_grads[a][(m // 4) * PASS : (m // 4 + 1) * PASS, :].rearrange("(w j) e -> j w e", j=4)
+            nc.sync.dma_start(out=rows[m % 4][:, cols], in_=results["dw", a, m][:, cols])
 
         V, A = "vector", "scalar"
         KEY, VAL = [(0, 0), (0, 1)], [(1, 0), (1, 1)]
+        load_w(0, 0)
         load_mean(0, 0)
         load_grad(0, 0, 0)
-        load_w(0, 0)
         load_grad(0, 0, 1)
         load_w(0, 1)
         load_mean(1, 0)
@@ -181,59 +202,62 @@ def tile_chunkedattention_pb_v_kernel(
         load_w(1, 0)
         load_grad(1, 0, 1)
         load_w(1, 1)
+        weave(A, "w", 0, 0, 1)
+        weave(V, "w", 0, 0, 0)
+        scale_mean(0, 0)
         load_mean(0, 1)
         load_grad(0, 1, 0)
         load_grad(0, 1, 1)
-        load_mean(1, 1)
-        scale_mean(0, 0)
+        quantize("w", 0, 0, 0)
         add(0, 0, 0)
-        load_grad(1, 1, 0)
         turn(0, 0, 0, 0, 0)
         drain(A, 0, 0, 0, 0)
-        weave(V, "w", 0, 0, 0)
+        add(0, 0, 1)
         turn(0, 0, 0, 1, 1)
         drain(A, 0, 0, 0, 1)
-        add(0, 0, 1)
-        load_grad(1, 1, 1)
-        turn(0, 0, 1, 0, 2)
-        weave(A, "w", 0, 0, 1)
-        quantize("w", 0, 0, 0)
-        load_x(0)
-        turn(0, 0, 1, 1, 3)
+        quantize("w", 0, 0, 1)
+        turn(0, 0, 1, 0, 0)
         drain(A, 0, 0, 1, 0)
+        weave(V, "tok", 0, 0, 0, halves=(0,))
+        turn(0, 0, 1, 1, 1)
+        drain(A, 0, 0, 1, 1)
         quantize("feat", 0, 0, 0)
         dx_passes(0, 0, 0, [(0, 0)], 4)
-        drain(A, 0, 0, 1, 1)
+        weave(A, "w", 0, 1, 1)
         weave(V, "w", 0, 1, 0)
         dx_passes(0, 1, 0, [(0, 0)], 5)
-        weave(A, "w", 0, 1, 1)
+        weave(A, "tok", 0, 0, 0, halves=(1,))
         scale_mean(1, 0)
+        load_mean(1, 1)
+        load_grad(1, 1, 0)
+        load_grad(1, 1, 1)
+        load_x(0)
         load_x(1)
         dx_passes(0, 2, 0, [(0, 0)], 6)
-        quantize("w", 0, 0, 1)
-        dx_passes(0, 3, 0, [(0, 0)], 7)
         add(1, 0, 0)
+        dx_passes(0, 3, 0, [(0, 0)], 7)
+        quantize("w", 0, 1, 0)
+        dx_passes(0, 0, 1, [(0, 0)], 2)
+        quantize("feat", 0, 0, 1)
+        dx_passes(0, 1, 1, [(0, 0)], 3)
+        weave(V, "w", 1, 0, 0)
         turn(1, 0, 0, 0, 0)
         drain(A, 1, 0, 0, 0)
-        quantize("w", 0, 1, 0)
+        quantize("w", 0, 1, 1)
         turn(1, 0, 0, 1, 1)
         drain(A, 1, 0, 0, 1)
-        quantize("feat", 0, 0, 1)
-        dx_passes(0, 0, 1, [(0, 0)], 2)
-        weave(A, "w", 1, 0, 1)
-        weave(V, "w", 1, 0, 0)
-        dx_passes(0, 1, 1, [(0, 0)], 3)
         add(1, 0, 1)
         dx_passes(0, 0, 0, [(0, 1)])
-        quantize("w", 0, 1, 1)
-        dx_passes(0, 1, 0, [(0, 1)])
+        weave(A, "w", 1, 0, 1)
         quantize("w", 1, 0, 0)
-        dx_passes(0, 2, 0, [(0, 1)])
+        dx_passes(0, 1, 0, [(0, 1)])
         quantize("feat", 1, 0, 0)
-        dx_passes(0, 3, 0, [(0, 1)])
+        dx_passes(0, 2, 0, [(0, 1)])
         weave(V, "w", 1, 1, 0)
-        dx_passes(0, 0, 1, [(0, 1)])
+        dx_passes(0, 3, 0, [(0, 1)])
         quantize("w", 1, 0, 1)
+        dx_passes(0, 0, 1, [(0, 1)])
+        quantize("w", 1, 1, 0)
         dx_passes(0, 1, 1, [(0, 1)])
         turn(1, 0, 1, 0, 0)
         drain(A, 1, 0, 1, 0)
@@ -242,20 +266,19 @@ def tile_chunkedattention_pb_v_kernel(
         quantize("feat", 1, 0, 1)
         dx_passes(0, 0, 0, [(1, 0)])
         weave(A, "w", 1, 1, 1)
-        quantize("w", 1, 1, 0)
-        dx_passes(0, 1, 0, [(1, 0)])
         scale_mean(0, 1)
-        dx_passes(0, 2, 0, [(1, 0)])
+        dx_passes(0, 1, 0, [(1, 0)])
         add(0, 1, 0)
-        dx_passes(0, 3, 0, [(1, 0)])
+        dx_passes(0, 2, 0, [(1, 0)])
         quantize("w", 1, 1, 1)
-        dx_passes(0, 0, 1, [(1, 0)])
+        dx_passes(0, 3, 0, [(1, 0)])
         add(0, 1, 1)
-        dx_passes(0, 1, 1, [(1, 0)])
+        dx_passes(0, 0, 1, [(1, 0)])
         scale_mean(1, 1)
+        dx_passes(0, 1, 1, [(1, 0)])
+        add(1, 1, 0)
         dx_passes(0, 0, 0, [(1, 1)])
         dx_out(A, 0, 0, 0)
-        add(1, 1, 0)
         dx_passes(0, 1, 0, [(1, 1)])
         dx_out(A, 0, 1, 0)
         dx_passes(0, 2, 0, [(1, 1)])
@@ -270,85 +293,84 @@ def tile_chunkedattention_pb_v_kernel(
         add(1, 1, 1)
         dx_passes(0, 1, 1, [(1, 1)])
         dx_out(A, 0, 3, 0)
+        quantize("tok", 0, 0, 0)
+        turn(0, 1, 1, 0, 0)
+        drain(A, 0, 1, 1, 0)
         weave(V, "x", 0, 0)
+        turn(0, 1, 1, 1, 1)
+        drain(A, 0, 1, 1, 1)
+        quantize("feat", 0, 1, 1)
         dx_passes(0, 2, 1, [(0, 0)], 4)
         dx_out(A, 0, 0, 1)
+        weave(V, "tok", 0, 1, 0)
         dx_store(0, 0)
         dx_passes(0, 2, 1, [(0, 1)])
         dx_out(A, 0, 1, 1)
         dx_store(0, 1)
         dx_passes(0, 2, 1, [(1, 0)])
         dx_passes(0, 2, 1, [(1, 1)])
-        turn(0, 1, 1, 0, 0)
-        drain(A, 0, 1, 1, 0)
-        turn(0, 1, 1, 1, 1)
-        drain(A, 0, 1, 1, 1)
-        quantize("feat", 0, 1, 1)
+        turn(1, 1, 0, 0, 0)
+        drain(A, 1, 1, 0, 0)
+        turn(1, 1, 0, 1, 1)
+        drain(A, 1, 1, 0, 1)
+        quantize("feat", 1, 1, 0)
         dx_passes(0, 3, 1, [(0, 0)], 5)
         dx_out(A, 0, 2, 1)
-        weave(V, "tok", 0, 0, 0)
         dx_store(0, 2)
         dx_passes(0, 3, 1, [(0, 1)])
         dx_passes(0, 3, 1, [(1, 0)])
         dx_passes(0, 3, 1, [(1, 1)])
         dx_out(A, 0, 3, 1)
         dx_store(0, 3)
-        turn(1, 1, 0, 0, 6)
-        drain(A, 1, 1, 0, 0)
-        turn(1, 1, 0, 1, 7)
-        drain(A, 1, 1, 0, 1)
-        quantize("feat", 1, 1, 0)
-        dx_passes(1, 0, 0, [(0, 0)], 2)
-        weave(V, "tok", 0, 1, 0)
-        dx_passes(1, 0, 1, [(0, 0)], 3)
         turn(1, 1, 1, 0, 0)
         drain(A, 1, 1, 1, 0)
         turn(1, 1, 1, 1, 1)
         drain(A, 1, 1, 1, 1)
         quantize("feat", 1, 1, 1)
-        dx_passes(1, 1, 0, [(0, 0)], 4)
+        dx_passes(1, 0, 0, [(0, 0)], 6)
         weave(A, "x", 0, 1)
-        quantize("tok", 0, 0, 0)
-        dx_passes(1, 1, 1, [(0, 0)], 5)
         weave(V, "x", 1, 0)
-        dx_passes(1, 0, 0, [(0, 1)])
+        dx_passes(1, 0, 1, [(0, 0)], 7)
         quantize("x", 0, 0)
-        dx_passes(1, 0, 1, [(0, 1)])
+        dx_passes(1, 1, 0, [(0, 0)], 2)
         weave(V, "x", 1, 1)
-        dx_passes(1, 1, 0, [(0, 1)])
+        dx_passes(1, 1, 1, [(0, 0)], 3)
         quantize("tok", 0, 1, 0)
-        dx_passes(1, 1, 1, [(0, 1)])
+        dx_passes(1, 0, 0, [(0, 1)])
         quantize("x", 1, 0)
-        dx_passes(1, 2, 0, [(0, 0)], 6)
+        dx_passes(1, 0, 1, [(0, 1)])
         quantize("x", 0, 1)
-        dx_passes(1, 2, 1, [(0, 0)], 7)
+        dx_passes(1, 1, 0, [(0, 1)])
         quantize("x", 1, 1)
-        dx_passes(1, 0, 0, [(1, 0)])
+        dx_passes(1, 1, 1, [(0, 1)])
         weave(V, "tok", 0, 0, 1)
-        dx_passes(1, 0, 0, [(1, 1)])
-        dx_out(A, 1, 0, 0)
+        dx_passes(1, 0, 0, [(1, 0)])
         weave(V, "tok", 0, 1, 1)
         dx_passes(1, 0, 1, [(1, 0)])
         quantize("tok", 0, 0, 1)
+        dx_passes(1, 1, 0, [(1, 0)])
+        weave(V, "tok", 1, 0, 0)
+        dx_passes(1, 1, 1, [(1, 0)])
+        quantize("tok", 0, 1, 1)
+        dx_passes(1, 0, 0, [(1, 1)])
+        dx_out(A, 1, 0, 0)
+        weave(V, "tok", 1, 1, 0)
         dx_passes(1, 0, 1, [(1, 1)])
         dx_out(A, 1, 0, 1)
-        weave(V, "tok", 1, 0, 0)
+        quantize("tok", 1, 0, 0)
         dx_store(1, 0)
-        dx_passes(1, 1, 0, [(1, 0)])
-        quantize("tok", 0, 1, 1)
         dx_passes(1, 1, 0, [(1, 1)])
         dx_out(A, 1, 1, 0)
-        weave(V, "tok", 1, 1, 0)
-        dx_passes(1, 1, 1, [(1, 0)])
-        quantize("tok", 1, 0, 0)
+        weave(V, "tok", 1, 0, 1)
         dx_passes(1, 1, 1, [(1, 1)])
         dx_out(A, 1, 1, 1)
-        weave(V, "tok", 1, 0, 1)
         dx_store(1, 1)
+        dx_passes(1, 2, 0, [(0, 0)], 4)
         dx_passes(1, 2, 0, [(0, 1)])
         dx_passes(1, 2, 0, [(1, 0)])
         dx_passes(1, 2, 0, [(1, 1)])
         dx_out(A, 1, 2, 0)
+        dx_passes(1, 2, 1, [(0, 0)], 5)
         dx_passes(1, 2, 1, [(0, 1)])
         dx_passes(1, 2, 1, [(1, 0)])
         dx_passes(1, 2, 1, [(1, 1)])
@@ -365,19 +387,19 @@ def tile_chunkedattention_pb_v_kernel(
         dx_passes(1, 3, 1, [(1, 1)])
         dx_out(A, 1, 3, 1)
         dx_store(1, 3)
-        dw_group(0, 0, 0, 2)
+        dw_group(0, 0, 0, 6)
         dw_out(A, 0, 0, 0)
-        dw_group(0, 0, 1, 3)
+        dw_group(0, 0, 1, 7)
         dw_out(A, 0, 0, 1)
         dw_store(0, 0)
-        dw_group(0, 1, 0, 4)
+        dw_group(0, 1, 0, 2)
         dw_out(A, 0, 1, 0)
-        dw_group(0, 1, 1, 5)
+        dw_group(0, 1, 1, 3)
         dw_out(A, 0, 1, 1)
         dw_store(0, 1)
-        dw_group(0, 2, 0, 6)
+        dw_group(0, 2, 0, 4)
         dw_out(A, 0, 2, 0)
-        dw_group(0, 2, 1, 7)
+        dw_group(0, 2, 1, 5)
         dw_out(A, 0, 2, 1)
         dw_store(0, 2)
         dw_group(0, 3, 0, 0)
@@ -386,21 +408,21 @@ def tile_chunkedattention_pb_v_kernel(
         dw_out(A, 0, 3, 1)
         quantize("tok", 1, 1, 0)
         dw_store(0, 3)
-        dw_group(0, 4, 0, 2)
+        dw_group(0, 4, 0, 6)
         dw_out(A, 0, 4, 0)
         weave(V, "tok", 1, 1, 1)
-        dw_group(0, 4, 1, 3)
+        dw_group(0, 4, 1, 7)
         dw_out(A, 0, 4, 1)
         quantize("tok", 1, 0, 1)
         dw_store(0, 4)
-        dw_group(0, 5, 0, 4)
+        dw_group(0, 5, 0, 2)
         dw_out(A, 0, 5, 0)
-        dw_group(0, 5, 1, 5)
+        dw_group(0, 5, 1, 3)
         dw_out(A, 0, 5, 1)
         dw_store(0, 5)
-        dw_group(0, 6, 0, 6)
+        dw_group(0, 6, 0, 4)
         dw_out(A, 0, 6, 0)
-        dw_group(0, 6, 1, 7)
+        dw_group(0, 6, 1, 5)
         dw_out(A, 0, 6, 1)
         dw_store(0, 6)
         dw_group(0, 7, 0, 0)
@@ -409,19 +431,19 @@ def tile_chunkedattention_pb_v_kernel(
         dw_out(A, 0, 7, 1)
         quantize("tok", 1, 1, 1)
         dw_store(0, 7)
-        dw_group(1, 0, 0, 2)
+        dw_group(1, 0, 0, 6)
         dw_out(A, 1, 0, 0)
-        dw_group(1, 0, 1, 3)
+        dw_group(1, 0, 1, 7)
         dw_out(A, 1, 0, 1)
         dw_store(1, 0)
-        dw_group(1, 1, 0, 4)
+        dw_group(1, 1, 0, 2)
         dw_out(A, 1, 1, 0)
-        dw_group(1, 1, 1, 5)
+        dw_group(1, 1, 1, 3)
         dw_out(V, 1, 1, 1)
         dw_store(1, 1)
-        dw_group(1, 2, 0, 6)
+        dw_group(1, 2, 0, 4)
         dw_out(A, 1, 2, 0)
-        dw_group(1, 2, 1, 7)
+        dw_group(1, 2, 1, 5)
         dw_out(V, 1, 2, 1)
         dw_store(1, 2)
         dw_group(1, 3, 0, 0)
@@ -429,23 +451,24 @@ def tile_chunkedattention_pb_v_kernel(
         dw_group(1, 3, 1, 1)
         dw_out(V, 1, 3, 1)
         dw_store(1, 3)
-        dw_group(1, 4, 0, 2)
+        dw_group(1, 4, 0, 6)
         dw_out(A, 1, 4, 0)
-        dw_group(1, 4, 1, 3)
+        dw_group(1, 4, 1, 7)
         dw_out(V, 1, 4, 1)
         dw_store(1, 4)
-        dw_group(1, 5, 0, 4)
+        dw_group(1, 5, 0, 2)
         dw_out(A, 1, 5, 0)
-        dw_group(1, 5, 1, 5)
+        dw_group(1, 5, 1, 3)
         dw_out(V, 1, 5, 1)
         dw_store(1, 5)
-        dw_group(1, 6, 0, 6)
+        dw_group(1, 6, 0, 4)
         dw_out(A, 1, 6, 0)
-        dw_group(1, 6, 1, 7)
+        dw_group(1, 6, 1, 5)
         dw_out(V, 1, 6, 1)
         dw_store(1, 6)
         dw_group(1, 7, 0, 0)
         dw_out(A, 1, 7, 0)
+        dw_store(1, 7, slice(0 * N, 1 * N))
         dw_group(1, 7, 1, 1)
         dw_out(V, 1, 7, 1)
-        dw_store(1, 7)
+        dw_store(1, 7, slice(1 * N, 2 * N))

@@ -5,7 +5,7 @@ from concourse.masks import make_identity
 
 S, E, H, D, T = 1024, 1024, 8, 128, 4
 FLOPS = 2 * S * E * E * 4
-BYTES = 2 * (3 * S * E + 2 * S * E + 2 * S * E // T) + 4 * 3 * S * E
+BYTES = 2 * (5 * S * E + 2 * S * E // T) + 4 * 3 * S * E
 
 F32 = mybir.dt.float32
 BF16 = mybir.dt.bfloat16
@@ -18,10 +18,15 @@ P = 128
 PACK = 4
 PASS = P * PACK
 N = 512
+HEADS = PASS // D
 RUN = 4
-LOADED, WIDE, TURNED, RESULTS = 6, 4, 3, 8
-WOVEN = {"vector": 4, "scalar": 2}
-CODES = {"w": 8, "x": 4, "feat": 8, "tok": 5}
+SHARED_FROM = (1, 1)
+
+WIDE_BUFS = 4
+TURNED_BUFS = 3
+WOVEN_BUFS = 6
+RESULT_BUFS = 8
+CODE_BUFS = {"w": 8, "x": 4, "feature": 8, "token": 5}
 
 
 def tile_chunkedattention_pb_v_kernel(
@@ -32,43 +37,41 @@ def tile_chunkedattention_pb_v_kernel(
     grads = (grad_0, grad_1)
     mean_grads = (grad_2, grad_3)
     weight_grads = (out_1, out_2)
+    on_vector, on_scalar = nc.vector.tensor_copy, nc.scalar.copy
 
     with ExitStack() as ctx:
-        keep = ctx.enter_context(tc.tile_pool(name="keep", bufs=1))
-        ring = ctx.enter_context(tc.tile_pool(name="ring", bufs=1))
+        sbuf = ctx.enter_context(tc.tile_pool(name="sbuf", bufs=1))
         psum = ctx.enter_context(tc.psum_pool(name="psum", bufs=1))
         ctx.enter_context(tc.manual_schedule())
 
-        ident = keep.tile([P, P], F32, name="ident")
+        ident = sbuf.tile([P, P], F32, name="ident")
         make_identity(nc, ident[:])
 
-        raw, banks, staged, mx, results = {}, {}, {}, {}, {}
+        means, loaded = {}, {}
+        rows = {}
+        staged = {}
+        mx = {}
+        banks = {}
+        results = {}
 
         def bank(index):
             return psum.tile([P, N], F32, name="bank", tag="bank%d" % index)
 
-        def copy(engine, out, in_):
-            if engine == "vector":
-                nc.vector.tensor_copy(out=out, in_=in_)
-            else:
-                nc.scalar.copy(out=out, in_=in_)
-
         def load_mean(a, g):
-            tile = ring.tile([P, H, D], BF16, name="mean", bufs=2)
-            nc.sync.dma_start(out=tile[:], in_=mean_grads[a][0, :, g * P : (g + 1) * P, :].rearrange("h p d -> p h d"))
-            raw["mean", a, g] = tile
+            means[a, g] = sbuf.tile([P, H, D], BF16, name="mean", bufs=4)
+            src = mean_grads[a][0, :, g * P : (g + 1) * P, :]
+            nc.sync.dma_start(out=means[a, g][:], in_=src.rearrange("h p d -> p h d"))
 
         def load_grad(a, g, c):
-            tile = ring.tile([P, 4, T * D], BF16, name="loaded", bufs=LOADED)
-            src = grads[a][0, 4 * c : 4 * c + 4, g * P : (g + 1) * P]
-            nc.sync.dma_start(out=tile[:], in_=src.rearrange("h p t d -> p h (t d)"))
-            raw["grad", a, g, c] = tile
+            loaded[a, g, c] = sbuf.tile([P, HEADS, T * D], BF16, name="grad", bufs=8)
+            src = grads[a][0, HEADS * c : HEADS * (c + 1), g * P : (g + 1) * P]
+            nc.sync.dma_start(out=loaded[a, g, c][:], in_=src.rearrange("h p t d -> p h (t d)"))
 
         def load_wide(key, src):
-            tile = ring.tile([P, PACK, E], BF16, name="wide", bufs=WIDE)
+            tile = sbuf.tile([P, PACK, E], BF16, name="wide", bufs=WIDE_BUFS)
             nc.sync.dma_start(out=tile[:], in_=src.rearrange("(p j) e -> p j e", j=PACK))
             for n in range(2):
-                raw[key + (n,)] = tile[:, :, n * N : (n + 1) * N]
+                rows[key + (n,)] = tile[:, :, n * N : (n + 1) * N]
 
         def load_w(a, c):
             load_wide(("w", a, c), weights[a][c * PASS : (c + 1) * PASS, :])
@@ -77,398 +80,205 @@ def tile_chunkedattention_pb_v_kernel(
             load_wide(("x", g), hidden_states[0, g * PASS : (g + 1) * PASS, :])
 
         def scale_mean(a, g):
-            tile = keep.tile([P, E], BF16, name="share", tag="share%d%d" % (a, g))
-            nc.vector.tensor_scalar(
-                out=tile[:].rearrange("p (u w e) -> p u w e", u=2, e=2),
-                in0=raw["mean", a, g][:].rearrange("p h (w u e) -> p u (h w) e", u=2, e=2),
-                scalar1=1.0 / T,
-                scalar2=None,
-                op0=mybir.AluOpType.mult,
-            )
-            raw["share", a, g] = tile
+            tile = means[a, g]
+            nc.vector.tensor_scalar(out=tile[:], in0=tile[:], scalar1=1.0 / T, scalar2=None, op0=mybir.AluOpType.mult)
 
-        def add(a, g, c):
-            tile = keep.tile([P, T * PASS], BF16, name="dy", tag="dy%d%d%d" % (a, g, c))
-            out = tile[:].rearrange("p (u t h w e) -> p u h t w e", u=2, t=T, h=4, e=2)
-            grad = raw["grad", a, g, c][:].rearrange("p h (t w u e) -> p u h t w e", t=T, u=2, e=2)
-            share = raw["share", a, g][:].rearrange("p (u h w e) -> p u h w e", u=2, h=H, e=2)
-            for u in range(2):
-                nc.vector.tensor_tensor(
-                    out=out[:, u],
-                    in0=grad[:, u],
-                    in1=share[:, u, 4 * c : 4 * c + 4].unsqueeze(2).to_broadcast([P, 4, T, 32, 2]),
-                    op=mybir.AluOpType.add,
+        def make_dy(a, g, c):
+            tile = sbuf.tile([P, T, PASS], BF16, name="dy", bufs=8)
+            nc.vector.tensor_tensor(
+                out=tile[:].rearrange("p t (h d) -> p h t d", d=D),
+                in0=loaded[a, g, c][:].rearrange("p h (t d) -> p h t d", d=D),
+                in1=means[a, g][:, HEADS * c : HEADS * (c + 1), :].unsqueeze(2).to_broadcast([P, HEADS, T, D]),
+                op=mybir.AluOpType.add,
+            )
+            rows["token", a, g, c] = tile[:]
+
+        def turn(a, g, c):
+            words = rows["token", a, g, c].rearrange("p t f -> p (t f)").bitcast(F32)
+            for i in range(2):
+                banks["turn", i] = bank(i)
+                for block in range(4):
+                    t, u = 2 * i + block // 2, block % 2
+                    nc.tensor.transpose(
+                        banks["turn", i][:, block * P : (block + 1) * P],
+                        words[:, 2 * P * t + u : 2 * P * (t + 1) : 2],
+                        ident[:],
+                    )
+
+        def drain(a, g, c):
+            tile = sbuf.tile([P, PACK * N], BF16, name="turned", bufs=TURNED_BUFS, align_bytes=64)
+            words = tile[:].bitcast(F32)
+            for i in range(2):
+                on_scalar(
+                    out=words[:, i * N : (i + 1) * N].rearrange("q (t p u) -> q t p u", t=2, u=2),
+                    in_=banks["turn", i][:].rearrange("q (t u p) -> q t p u", t=2, u=2),
                 )
-            raw["tok", a, g, c] = tile[:]
+            staged["feature", a, g, c] = tile
 
-        def turn(a, g, c, half, index):
-            words = raw["tok", a, g, c].bitcast(F32)
-            tile = bank(index)
-            for i in range(4):
-                block = T * (i % 2) + 2 * half + i // 2
-                nc.tensor.transpose(tile[:, i * P : (i + 1) * P], words[:, block * P : (block + 1) * P], ident[:])
-            banks["turn", a, g, c, half] = tile
-
-        def drain(engine, a, g, c, half):
-            if half == 0:
-                staged["feat", a, g, c] = ring.tile([P, 4 * N], BF16, name="turned", bufs=TURNED, align_bytes=64)
-            words = staged["feat", a, g, c][:].bitcast(F32)
+        def weave(copy, key):
+            staged[key] = sbuf.tile([P, PACK * N], BF16, name="woven", bufs=WOVEN_BUFS, align_bytes=64)
             copy(
-                engine,
-                words[:, half * N : (half + 1) * N].rearrange("q (t p u) -> q t p u", t=2, u=2),
-                banks["turn", a, g, c, half][:].rearrange("q (t u p) -> q t p u", t=2, u=2),
+                out=staged[key][:].rearrange("p (f i j) -> p f j i", j=PACK, i=RUN),
+                in_=rows[key].rearrange("p j (f i) -> p f j i", i=RUN),
             )
 
-        def interleave(engine, dst, src):
-            copy(
-                engine,
-                dst.rearrange("p (c i t) -> p c t i", t=PACK, i=RUN),
-                src.rearrange("p t (c i) -> p c t i", i=RUN),
-            )
-
-        def weave(engine, *key, halves=(0, 1)):
-            if halves[0] == 0:
-                staged[key] = ring.tile([P, 4 * N], BF16, name="woven", tag="woven" + engine, bufs=WOVEN[engine], align_bytes=64)
-            tile = staged[key]
-            lo, hi = halves[0], halves[-1] + 1
-            if key[0] == "tok":
-                copy(
-                    engine,
-                    tile[:].rearrange("p (u e w t) -> p u w t e", u=2, e=2, t=PACK)[:, lo:hi],
-                    raw[key].rearrange("p (u t w e) -> p u w t e", u=2, t=PACK, e=2)[:, lo:hi],
-                )
-            else:
-                interleave(engine, tile[:, lo * 2 * N : hi * 2 * N], raw[key][:, :, lo * 256 : hi * 256])
-
-        def quantize(*key):
+        def quantize(key):
             kind = key[0]
-            codes = ring.tile([P, N], U32, name="codes", tag="codes_" + kind, bufs=CODES[kind], align_bytes=64)
-            scales = ring.tile([P, N], U8, name="scales", tag="scales_" + kind, bufs=CODES[kind], align_bytes=64)
-            fmt = E5M2 if key[0] in ("feat", "tok") else E4M3
+            codes = sbuf.tile([P, N], U32, name="codes_" + kind, bufs=CODE_BUFS[kind], align_bytes=64)
+            scales = sbuf.tile([P, N], U8, name="scales_" + kind, bufs=CODE_BUFS[kind], align_bytes=64)
+            fmt = E4M3 if kind in ("w", "x") else E5M2
             nc.vector.quantize_mx(out=codes[:].bitcast(fmt), scales=scales[:], in_=staged[key][:])
             mx[key] = (codes, scales)
 
-        def matmul(acc, lhs, column, rhs, start, stop):
-            cols = slice(column, column + P)
+        def matmul(acc, dy_key, block, other_key, start, stop):
+            cols = slice(block * P, (block + 1) * P)
             nc.tensor.matmul_mx(
                 out=acc[:],
-                lhsT=mx[lhs][0][:, cols].bitcast(E5M2),
-                lhsT_scale=mx[lhs][1][:, cols],
-                rhs=mx[rhs][0][:].bitcast(E4M3),
-                rhs_scale=mx[rhs][1][:],
+                lhsT=mx[dy_key][0][:, cols].bitcast(E5M2),
+                lhsT_scale=mx[dy_key][1][:, cols],
+                rhs=mx[other_key][0][:].bitcast(E4M3),
+                rhs_scale=mx[other_key][1][:],
                 start=start,
                 stop=stop,
             )
 
-        def dx_passes(g, t, n, passes, index=None):
-            if index is not None:
+        steps = [(a, c) for a in range(2) for c in range(2)]
+
+        def dx_pass(g, t, n, step, index):
+            if step == steps[0]:
                 banks["dx", g, t, n] = bank(index)
-            for a, c in passes:
-                matmul(banks["dx", g, t, n], ("feat", a, g, c), t * P, ("w", a, c, n), (a, c) == (0, 0), (a, c) == (1, 1))
+            a, c = step
+            matmul(banks["dx", g, t, n], ("feature", a, g, c), t, ("w", a, c, n), step == steps[0], step == steps[-1])
 
-        def dx_out(engine, g, t, n):
-            if n == 0:
-                results["dx", g, t] = ring.tile([P, E], F32, name="result", bufs=RESULTS)
-            copy(engine, results["dx", g, t][:, n * N : (n + 1) * N], banks["dx", g, t, n][:])
-
-        def dx_store(g, t):
-            rows = out_0[0, g * PASS : (g + 1) * PASS, :].rearrange("(p t) e -> t p e", t=T)
-            nc.sync.dma_start(out=rows[t], in_=results["dx", g, t][:])
+        def dx_group(g, t, n, index):
+            for step in steps:
+                dx_pass(g, t, n, step, index)
 
         def dw_group(a, m, n, index):
-            acc = bank(index)
+            banks["dw", a, m, n] = bank(index)
             for g in range(2):
-                matmul(acc, ("tok", a, g, m // 4), (m % 4) * P, ("x", g, n), g == 0, g == 1)
-            banks["dw", a, m, n] = acc
+                matmul(banks["dw", a, m, n], ("token", a, g, m // HEADS), m % HEADS, ("x", g, n), g == 0, g == 1)
 
-        def dw_out(engine, a, m, n):
+        def copy_out(copy, key, n):
             if n == 0:
-                results["dw", a, m] = ring.tile([P, E], F32, name="result", bufs=RESULTS)
-            copy(engine, results["dw", a, m][:, n * N : (n + 1) * N], banks["dw", a, m, n][:])
+                results[key] = sbuf.tile([P, E], F32, name="result", bufs=RESULT_BUFS)
+            copy(out=results[key][:, n * N : (n + 1) * N], in_=banks[key + (n,)][:])
 
-        def dw_store(a, m, cols=slice(0, E)):
-            rows = weight_grads[a][(m // 4) * PASS : (m // 4 + 1) * PASS, :].rearrange("(w j) e -> j w e", j=4)
-            nc.sync.dma_start(out=rows[m % 4][:, cols], in_=results["dw", a, m][:, cols])
+        def store_dx(g, t):
+            dst = out_0[0, g * PASS : (g + 1) * PASS, :].rearrange("(p t) e -> t p e", t=T)
+            nc.sync.dma_start(out=dst[t], in_=results["dx", g, t][:])
 
-        V, A = "vector", "scalar"
-        KEY, VAL = [(0, 0), (0, 1)], [(1, 0), (1, 1)]
-        load_w(0, 0)
-        load_mean(0, 0)
-        load_grad(0, 0, 0)
-        load_grad(0, 0, 1)
-        load_w(0, 1)
-        load_mean(1, 0)
-        load_grad(1, 0, 0)
-        load_w(1, 0)
-        load_grad(1, 0, 1)
-        load_w(1, 1)
-        weave(A, "w", 0, 0, 1)
-        weave(V, "w", 0, 0, 0)
+        def store_dw(a, m, cols):
+            nc.sync.dma_start(out=weight_grads[a][m * P : (m + 1) * P, cols], in_=results["dw", a, m][:, cols])
+
+        for g in range(2):
+            for a, c in steps:
+                if c == 0:
+                    load_mean(a, g)
+                load_grad(a, g, c)
+                if g == 0:
+                    load_w(a, c)
+
+        early = [(0, 0, 4), (1, 0, 5), (2, 0, 6), (3, 0, 7), (0, 1, 2), (1, 1, 3)]
         scale_mean(0, 0)
-        load_mean(0, 1)
-        load_grad(0, 1, 0)
-        load_grad(0, 1, 1)
-        quantize("w", 0, 0, 0)
-        add(0, 0, 0)
-        turn(0, 0, 0, 0, 0)
-        drain(A, 0, 0, 0, 0)
-        add(0, 0, 1)
-        turn(0, 0, 0, 1, 1)
-        drain(A, 0, 0, 0, 1)
-        quantize("w", 0, 0, 1)
-        turn(0, 0, 1, 0, 0)
-        drain(A, 0, 0, 1, 0)
-        weave(V, "tok", 0, 0, 0, halves=(0,))
-        turn(0, 0, 1, 1, 1)
-        drain(A, 0, 0, 1, 1)
-        quantize("feat", 0, 0, 0)
-        dx_passes(0, 0, 0, [(0, 0)], 4)
-        weave(A, "w", 0, 1, 1)
-        weave(V, "w", 0, 1, 0)
-        dx_passes(0, 1, 0, [(0, 0)], 5)
-        weave(A, "tok", 0, 0, 0, halves=(1,))
-        scale_mean(1, 0)
-        load_mean(1, 1)
-        load_grad(1, 1, 0)
-        load_grad(1, 1, 1)
-        load_x(0)
-        load_x(1)
-        dx_passes(0, 2, 0, [(0, 0)], 6)
-        add(1, 0, 0)
-        dx_passes(0, 3, 0, [(0, 0)], 7)
-        quantize("w", 0, 1, 0)
-        dx_passes(0, 0, 1, [(0, 0)], 2)
-        quantize("feat", 0, 0, 1)
-        dx_passes(0, 1, 1, [(0, 0)], 3)
-        weave(V, "w", 1, 0, 0)
-        turn(1, 0, 0, 0, 0)
-        drain(A, 1, 0, 0, 0)
-        quantize("w", 0, 1, 1)
-        turn(1, 0, 0, 1, 1)
-        drain(A, 1, 0, 0, 1)
-        add(1, 0, 1)
-        dx_passes(0, 0, 0, [(0, 1)])
-        weave(A, "w", 1, 0, 1)
-        quantize("w", 1, 0, 0)
-        dx_passes(0, 1, 0, [(0, 1)])
-        quantize("feat", 1, 0, 0)
-        dx_passes(0, 2, 0, [(0, 1)])
-        weave(V, "w", 1, 1, 0)
-        dx_passes(0, 3, 0, [(0, 1)])
-        quantize("w", 1, 0, 1)
-        dx_passes(0, 0, 1, [(0, 1)])
-        quantize("w", 1, 1, 0)
-        dx_passes(0, 1, 1, [(0, 1)])
-        turn(1, 0, 1, 0, 0)
-        drain(A, 1, 0, 1, 0)
-        turn(1, 0, 1, 1, 1)
-        drain(A, 1, 0, 1, 1)
-        quantize("feat", 1, 0, 1)
-        dx_passes(0, 0, 0, [(1, 0)])
-        weave(A, "w", 1, 1, 1)
-        scale_mean(0, 1)
-        dx_passes(0, 1, 0, [(1, 0)])
-        add(0, 1, 0)
-        dx_passes(0, 2, 0, [(1, 0)])
-        quantize("w", 1, 1, 1)
-        dx_passes(0, 3, 0, [(1, 0)])
-        add(0, 1, 1)
-        dx_passes(0, 0, 1, [(1, 0)])
+        for before, (a, c) in zip([None] + steps, steps):
+            make_dy(a, 0, c)
+            turn(a, 0, c)
+            drain(a, 0, c)
+            if before:
+                quantize(("w",) + before + (0,))
+                quantize(("feature", before[0], 0, before[1]))
+            weave(on_vector, ("w", a, c, 0))
+            weave(on_scalar, ("w", a, c, 1))
+            if c == 1:
+                scale_mean(1 - a, a)
+            if before:
+                quantize(("w",) + before + (1,))
+                for t, n, index in early:
+                    dx_pass(0, t, n, before, index)
+            if a == 1:
+                load_x(c)
+        quantize(("feature", 1, 0, 1))
+        quantize(("w", 1, 1, 0))
+        for t, n, index in early[:4]:
+            dx_pass(0, t, n, steps[-1], index)
+
+        make_dy(0, 1, 0)
+        quantize(("w", 1, 1, 1))
+        turn(0, 1, 0)
+        for t, n, index in early[4:]:
+            dx_pass(0, t, n, steps[-1], index)
+        copy_out(on_scalar, ("dx", 0, 0), 0)
+        copy_out(on_scalar, ("dx", 0, 1), 0)
+        drain(0, 1, 0)
+
+        make_dy(0, 1, 1)
         scale_mean(1, 1)
-        dx_passes(0, 1, 1, [(1, 0)])
-        add(1, 1, 0)
-        dx_passes(0, 0, 0, [(1, 1)])
-        dx_out(A, 0, 0, 0)
-        dx_passes(0, 1, 0, [(1, 1)])
-        dx_out(A, 0, 1, 0)
-        dx_passes(0, 2, 0, [(1, 1)])
-        dx_passes(0, 3, 0, [(1, 1)])
-        turn(0, 1, 0, 0, 0)
-        drain(A, 0, 1, 0, 0)
-        turn(0, 1, 0, 1, 1)
-        drain(A, 0, 1, 0, 1)
-        quantize("feat", 0, 1, 0)
-        dx_passes(0, 0, 1, [(1, 1)])
-        dx_out(A, 0, 2, 0)
-        add(1, 1, 1)
-        dx_passes(0, 1, 1, [(1, 1)])
-        dx_out(A, 0, 3, 0)
-        quantize("tok", 0, 0, 0)
-        turn(0, 1, 1, 0, 0)
-        drain(A, 0, 1, 1, 0)
-        weave(V, "x", 0, 0)
-        turn(0, 1, 1, 1, 1)
-        drain(A, 0, 1, 1, 1)
-        quantize("feat", 0, 1, 1)
-        dx_passes(0, 2, 1, [(0, 0)], 4)
-        dx_out(A, 0, 0, 1)
-        weave(V, "tok", 0, 1, 0)
-        dx_store(0, 0)
-        dx_passes(0, 2, 1, [(0, 1)])
-        dx_out(A, 0, 1, 1)
-        dx_store(0, 1)
-        dx_passes(0, 2, 1, [(1, 0)])
-        dx_passes(0, 2, 1, [(1, 1)])
-        turn(1, 1, 0, 0, 0)
-        drain(A, 1, 1, 0, 0)
-        turn(1, 1, 0, 1, 1)
-        drain(A, 1, 1, 0, 1)
-        quantize("feat", 1, 1, 0)
-        dx_passes(0, 3, 1, [(0, 0)], 5)
-        dx_out(A, 0, 2, 1)
-        dx_store(0, 2)
-        dx_passes(0, 3, 1, [(0, 1)])
-        dx_passes(0, 3, 1, [(1, 0)])
-        dx_passes(0, 3, 1, [(1, 1)])
-        dx_out(A, 0, 3, 1)
-        dx_store(0, 3)
-        turn(1, 1, 1, 0, 0)
-        drain(A, 1, 1, 1, 0)
-        turn(1, 1, 1, 1, 1)
-        drain(A, 1, 1, 1, 1)
-        quantize("feat", 1, 1, 1)
-        dx_passes(1, 0, 0, [(0, 0)], 6)
-        weave(A, "x", 0, 1)
-        weave(V, "x", 1, 0)
-        dx_passes(1, 0, 1, [(0, 0)], 7)
-        quantize("x", 0, 0)
-        dx_passes(1, 1, 0, [(0, 0)], 2)
-        weave(V, "x", 1, 1)
-        dx_passes(1, 1, 1, [(0, 0)], 3)
-        quantize("tok", 0, 1, 0)
-        dx_passes(1, 0, 0, [(0, 1)])
-        quantize("x", 1, 0)
-        dx_passes(1, 0, 1, [(0, 1)])
-        quantize("x", 0, 1)
-        dx_passes(1, 1, 0, [(0, 1)])
-        quantize("x", 1, 1)
-        dx_passes(1, 1, 1, [(0, 1)])
-        weave(V, "tok", 0, 0, 1)
-        dx_passes(1, 0, 0, [(1, 0)])
-        weave(V, "tok", 0, 1, 1)
-        dx_passes(1, 0, 1, [(1, 0)])
-        quantize("tok", 0, 0, 1)
-        dx_passes(1, 1, 0, [(1, 0)])
-        weave(V, "tok", 1, 0, 0)
-        dx_passes(1, 1, 1, [(1, 0)])
-        quantize("tok", 0, 1, 1)
-        dx_passes(1, 0, 0, [(1, 1)])
-        dx_out(A, 1, 0, 0)
-        weave(V, "tok", 1, 1, 0)
-        dx_passes(1, 0, 1, [(1, 1)])
-        dx_out(A, 1, 0, 1)
-        quantize("tok", 1, 0, 0)
-        dx_store(1, 0)
-        dx_passes(1, 1, 0, [(1, 1)])
-        dx_out(A, 1, 1, 0)
-        weave(V, "tok", 1, 0, 1)
-        dx_passes(1, 1, 1, [(1, 1)])
-        dx_out(A, 1, 1, 1)
-        dx_store(1, 1)
-        dx_passes(1, 2, 0, [(0, 0)], 4)
-        dx_passes(1, 2, 0, [(0, 1)])
-        dx_passes(1, 2, 0, [(1, 0)])
-        dx_passes(1, 2, 0, [(1, 1)])
-        dx_out(A, 1, 2, 0)
-        dx_passes(1, 2, 1, [(0, 0)], 5)
-        dx_passes(1, 2, 1, [(0, 1)])
-        dx_passes(1, 2, 1, [(1, 0)])
-        dx_passes(1, 2, 1, [(1, 1)])
-        dx_out(A, 1, 2, 1)
-        dx_store(1, 2)
-        dx_passes(1, 3, 0, [(0, 0)], 0)
-        dx_passes(1, 3, 0, [(0, 1)])
-        dx_passes(1, 3, 0, [(1, 0)])
-        dx_passes(1, 3, 0, [(1, 1)])
-        dx_out(A, 1, 3, 0)
-        dx_passes(1, 3, 1, [(0, 0)], 1)
-        dx_passes(1, 3, 1, [(0, 1)])
-        dx_passes(1, 3, 1, [(1, 0)])
-        dx_passes(1, 3, 1, [(1, 1)])
-        dx_out(A, 1, 3, 1)
-        dx_store(1, 3)
-        dw_group(0, 0, 0, 6)
-        dw_out(A, 0, 0, 0)
-        dw_group(0, 0, 1, 7)
-        dw_out(A, 0, 0, 1)
-        dw_store(0, 0)
-        dw_group(0, 1, 0, 2)
-        dw_out(A, 0, 1, 0)
-        dw_group(0, 1, 1, 3)
-        dw_out(A, 0, 1, 1)
-        dw_store(0, 1)
-        dw_group(0, 2, 0, 4)
-        dw_out(A, 0, 2, 0)
-        dw_group(0, 2, 1, 5)
-        dw_out(A, 0, 2, 1)
-        dw_store(0, 2)
-        dw_group(0, 3, 0, 0)
-        dw_out(A, 0, 3, 0)
-        dw_group(0, 3, 1, 1)
-        dw_out(A, 0, 3, 1)
-        quantize("tok", 1, 1, 0)
-        dw_store(0, 3)
-        dw_group(0, 4, 0, 6)
-        dw_out(A, 0, 4, 0)
-        weave(V, "tok", 1, 1, 1)
-        dw_group(0, 4, 1, 7)
-        dw_out(A, 0, 4, 1)
-        quantize("tok", 1, 0, 1)
-        dw_store(0, 4)
-        dw_group(0, 5, 0, 2)
-        dw_out(A, 0, 5, 0)
-        dw_group(0, 5, 1, 3)
-        dw_out(A, 0, 5, 1)
-        dw_store(0, 5)
-        dw_group(0, 6, 0, 4)
-        dw_out(A, 0, 6, 0)
-        dw_group(0, 6, 1, 5)
-        dw_out(A, 0, 6, 1)
-        dw_store(0, 6)
-        dw_group(0, 7, 0, 0)
-        dw_out(A, 0, 7, 0)
-        dw_group(0, 7, 1, 1)
-        dw_out(A, 0, 7, 1)
-        quantize("tok", 1, 1, 1)
-        dw_store(0, 7)
-        dw_group(1, 0, 0, 6)
-        dw_out(A, 1, 0, 0)
-        dw_group(1, 0, 1, 7)
-        dw_out(A, 1, 0, 1)
-        dw_store(1, 0)
-        dw_group(1, 1, 0, 2)
-        dw_out(A, 1, 1, 0)
-        dw_group(1, 1, 1, 3)
-        dw_out(V, 1, 1, 1)
-        dw_store(1, 1)
-        dw_group(1, 2, 0, 4)
-        dw_out(A, 1, 2, 0)
-        dw_group(1, 2, 1, 5)
-        dw_out(V, 1, 2, 1)
-        dw_store(1, 2)
-        dw_group(1, 3, 0, 0)
-        dw_out(A, 1, 3, 0)
-        dw_group(1, 3, 1, 1)
-        dw_out(V, 1, 3, 1)
-        dw_store(1, 3)
-        dw_group(1, 4, 0, 6)
-        dw_out(A, 1, 4, 0)
-        dw_group(1, 4, 1, 7)
-        dw_out(V, 1, 4, 1)
-        dw_store(1, 4)
-        dw_group(1, 5, 0, 2)
-        dw_out(A, 1, 5, 0)
-        dw_group(1, 5, 1, 3)
-        dw_out(V, 1, 5, 1)
-        dw_store(1, 5)
-        dw_group(1, 6, 0, 4)
-        dw_out(A, 1, 6, 0)
-        dw_group(1, 6, 1, 5)
-        dw_out(V, 1, 6, 1)
-        dw_store(1, 6)
-        dw_group(1, 7, 0, 0)
-        dw_out(A, 1, 7, 0)
-        dw_store(1, 7, slice(0 * N, 1 * N))
-        dw_group(1, 7, 1, 1)
-        dw_out(V, 1, 7, 1)
-        dw_store(1, 7, slice(1 * N, 2 * N))
+        turn(0, 1, 1)
+        dx_group(0, 2, 1, 4)
+        copy_out(on_scalar, ("dx", 0, 2), 0)
+        copy_out(on_scalar, ("dx", 0, 3), 0)
+        drain(0, 1, 1)
+
+        make_dy(1, 1, 0)
+        quantize(("feature", 0, 1, 0))
+        turn(1, 1, 0)
+        dx_group(0, 3, 1, 5)
+        copy_out(on_scalar, ("dx", 0, 0), 1)
+        copy_out(on_scalar, ("dx", 0, 1), 1)
+        drain(1, 1, 0)
+
+        make_dy(1, 1, 1)
+        turn(1, 1, 1)
+        copy_out(on_scalar, ("dx", 0, 2), 1)
+        copy_out(on_scalar, ("dx", 0, 3), 1)
+        drain(1, 1, 1)
+        for t in range(T):
+            store_dx(0, t)
+
+        weave(on_vector, ("x", 0, 0))
+        weave(on_scalar, ("x", 0, 1))
+        quantize(("feature", 0, 1, 1))
+        weave(on_vector, ("token", 0, 0, 0))
+        quantize(("feature", 1, 1, 0))
+        weave(on_vector, ("token", 0, 1, 0))
+        quantize(("feature", 1, 1, 1))
+        quantize(("token", 0, 0, 0))
+
+        order = [6, 7, 2, 3, 4, 5, 0, 1]
+        late = [(t, n, order[2 * t + n]) for t in range(T) for n in range(2)]
+        for step in steps:
+            for t, n, index in late[:4]:
+                dx_pass(1, t, n, step, index)
+        for t, n, index in late[4:]:
+            dx_group(1, t, n, index)
+        for t in range(T):
+            copy_out(on_scalar, ("dx", 1, t), 0)
+            copy_out(on_scalar, ("dx", 1, t), 1)
+            store_dx(1, t)
+
+        weave(on_vector, ("x", 1, 0))
+        quantize(("x", 0, 0))
+        weave(on_vector, ("x", 1, 1))
+        quantize(("token", 0, 1, 0))
+        quantize(("x", 1, 0))
+        quantize(("x", 0, 1))
+        quantize(("x", 1, 1))
+
+        tokens = [("token", a, g, c) for a, c in steps for g in range(2)]
+        weave(on_vector, tokens[2])
+        for i, (a, c) in enumerate(steps):
+            for k in range(2 * i + 2, min(2 * i + 4, len(tokens))):
+                if k + 1 < len(tokens):
+                    weave(on_vector, tokens[k + 1])
+                quantize(tokens[k])
+            for m in range(HEADS * c, HEADS * (c + 1)):
+                shared = (a, m) >= SHARED_FROM
+                for n in range(2):
+                    dw_group(a, m, n, order[(2 * m + n) % len(order)])
+                    copy_out(on_vector if shared and n == 1 else on_scalar, ("dw", a, m), n)
+                if (a, m) == (1, H - 1):
+                    store_dw(a, m, slice(0, N))
+                    store_dw(a, m, slice(N, E))
+                else:
+                    store_dw(a, m, slice(0, E))

from contextlib import ExitStack

import concourse.mybir as mybir
from concourse.masks import make_identity

S, E, H, D, T = 1024, 1024, 8, 128, 4
FLOPS = 2 * S * E * E * 4
BYTES = 2 * (5 * S * E + 2 * S * E // T) + 4 * 3 * S * E

F32 = mybir.dt.float32
BF16 = mybir.dt.bfloat16
U32 = mybir.dt.uint32
U8 = mybir.dt.uint8
E4M3 = mybir.dt.float8_e4m3fn_x4
E5M2 = mybir.dt.float8_e5m2_x4

P = 128
PACK = 4
PASS = P * PACK
N = 512
HEADS = PASS // D
RUN = 4
SHARED_FROM = (1, 1)

WIDE_BUFS = 4
TURNED_BUFS = 3
WOVEN_BUFS = 6
RESULT_BUFS = 8
CODE_BUFS = {"w": 8, "x": 4, "feature": 8, "token": 5}


def tile_chunkedattention_pb_v_kernel(
    tc, hidden_states, wk, bk, wv, bv, grad_0, grad_1, grad_2, grad_3, out_0, out_1, out_2
):
    nc = tc.nc
    weights = (wk, wv)
    grads = (grad_0, grad_1)
    mean_grads = (grad_2, grad_3)
    weight_grads = (out_1, out_2)
    on_vector, on_scalar = nc.vector.tensor_copy, nc.scalar.copy

    with ExitStack() as ctx:
        sbuf = ctx.enter_context(tc.tile_pool(name="sbuf", bufs=1))
        psum = ctx.enter_context(tc.psum_pool(name="psum", bufs=1))
        ctx.enter_context(tc.manual_schedule())

        ident = sbuf.tile([P, P], F32, name="ident")
        make_identity(nc, ident[:])

        means, loaded = {}, {}
        rows = {}
        staged = {}
        mx = {}
        banks = {}
        results = {}

        def bank(index):
            return psum.tile([P, N], F32, name="bank", tag="bank%d" % index)

        def load_mean(a, g):
            means[a, g] = sbuf.tile([P, H, D], BF16, name="mean", bufs=4)
            src = mean_grads[a][0, :, g * P : (g + 1) * P, :]
            nc.sync.dma_start(out=means[a, g][:], in_=src.rearrange("h p d -> p h d"))

        def load_grad(a, g, c):
            loaded[a, g, c] = sbuf.tile([P, HEADS, T * D], BF16, name="grad", bufs=8)
            src = grads[a][0, HEADS * c : HEADS * (c + 1), g * P : (g + 1) * P]
            nc.sync.dma_start(out=loaded[a, g, c][:], in_=src.rearrange("h p t d -> p h (t d)"))

        def load_wide(key, src):
            tile = sbuf.tile([P, PACK, E], BF16, name="wide", bufs=WIDE_BUFS)
            nc.sync.dma_start(out=tile[:], in_=src.rearrange("(p j) e -> p j e", j=PACK))
            for n in range(2):
                rows[key + (n,)] = tile[:, :, n * N : (n + 1) * N]

        def load_w(a, c):
            load_wide(("w", a, c), weights[a][c * PASS : (c + 1) * PASS, :])

        def load_x(g):
            load_wide(("x", g), hidden_states[0, g * PASS : (g + 1) * PASS, :])

        def scale_mean(a, g):
            tile = means[a, g]
            nc.vector.tensor_scalar(out=tile[:], in0=tile[:], scalar1=1.0 / T, scalar2=None, op0=mybir.AluOpType.mult)

        def make_dy(a, g, c):
            tile = sbuf.tile([P, T, PASS], BF16, name="dy", bufs=8)
            nc.vector.tensor_tensor(
                out=tile[:].rearrange("p t (h d) -> p h t d", d=D),
                in0=loaded[a, g, c][:].rearrange("p h (t d) -> p h t d", d=D),
                in1=means[a, g][:, HEADS * c : HEADS * (c + 1), :].unsqueeze(2).to_broadcast([P, HEADS, T, D]),
                op=mybir.AluOpType.add,
            )
            rows["token", a, g, c] = tile[:]

        def turn(a, g, c):
            words = rows["token", a, g, c].rearrange("p t f -> p (t f)").bitcast(F32)
            for i in range(2):
                banks["turn", i] = bank(i)
                for block in range(4):
                    t, u = 2 * i + block // 2, block % 2
                    nc.tensor.transpose(
                        banks["turn", i][:, block * P : (block + 1) * P],
                        words[:, 2 * P * t + u : 2 * P * (t + 1) : 2],
                        ident[:],
                    )

        def drain(a, g, c):
            tile = sbuf.tile([P, PACK * N], BF16, name="turned", bufs=TURNED_BUFS, align_bytes=64)
            words = tile[:].bitcast(F32)
            for i in range(2):
                on_scalar(
                    out=words[:, i * N : (i + 1) * N].rearrange("q (t p u) -> q t p u", t=2, u=2),
                    in_=banks["turn", i][:].rearrange("q (t u p) -> q t p u", t=2, u=2),
                )
            staged["feature", a, g, c] = tile

        def weave(copy, key):
            staged[key] = sbuf.tile([P, PACK * N], BF16, name="woven", bufs=WOVEN_BUFS, align_bytes=64)
            copy(
                out=staged[key][:].rearrange("p (f i j) -> p f j i", j=PACK, i=RUN),
                in_=rows[key].rearrange("p j (f i) -> p f j i", i=RUN),
            )

        def quantize(key):
            kind = key[0]
            codes = sbuf.tile([P, N], U32, name="codes_" + kind, bufs=CODE_BUFS[kind], align_bytes=64)
            scales = sbuf.tile([P, N], U8, name="scales_" + kind, bufs=CODE_BUFS[kind], align_bytes=64)
            fmt = E4M3 if kind in ("w", "x") else E5M2
            nc.vector.quantize_mx(out=codes[:].bitcast(fmt), scales=scales[:], in_=staged[key][:])
            mx[key] = (codes, scales)

        def matmul(acc, dy_key, block, other_key, start, stop):
            cols = slice(block * P, (block + 1) * P)
            nc.tensor.matmul_mx(
                out=acc[:],
                lhsT=mx[dy_key][0][:, cols].bitcast(E5M2),
                lhsT_scale=mx[dy_key][1][:, cols],
                rhs=mx[other_key][0][:].bitcast(E4M3),
                rhs_scale=mx[other_key][1][:],
                start=start,
                stop=stop,
            )

        steps = [(a, c) for a in range(2) for c in range(2)]

        def dx_pass(g, t, n, step, index):
            if step == steps[0]:
                banks["dx", g, t, n] = bank(index)
            a, c = step
            matmul(banks["dx", g, t, n], ("feature", a, g, c), t, ("w", a, c, n), step == steps[0], step == steps[-1])

        def dx_group(g, t, n, index):
            for step in steps:
                dx_pass(g, t, n, step, index)

        def dw_group(a, m, n, index):
            banks["dw", a, m, n] = bank(index)
            for g in range(2):
                matmul(banks["dw", a, m, n], ("token", a, g, m // HEADS), m % HEADS, ("x", g, n), g == 0, g == 1)

        def copy_out(copy, key, n):
            if n == 0:
                results[key] = sbuf.tile([P, E], F32, name="result", bufs=RESULT_BUFS)
            copy(out=results[key][:, n * N : (n + 1) * N], in_=banks[key + (n,)][:])

        def store_dx(g, t):
            dst = out_0[0, g * PASS : (g + 1) * PASS, :].rearrange("(p t) e -> t p e", t=T)
            nc.sync.dma_start(out=dst[t], in_=results["dx", g, t][:])

        def store_dw(a, m, cols):
            nc.sync.dma_start(out=weight_grads[a][m * P : (m + 1) * P, cols], in_=results["dw", a, m][:, cols])

        for g in range(2):
            for a, c in steps:
                if c == 0:
                    load_mean(a, g)
                load_grad(a, g, c)
                if g == 0:
                    load_w(a, c)

        early = [(0, 0, 4), (1, 0, 5), (2, 0, 6), (3, 0, 7), (0, 1, 2), (1, 1, 3)]
        scale_mean(0, 0)
        for before, (a, c) in zip([None] + steps, steps):
            make_dy(a, 0, c)
            turn(a, 0, c)
            drain(a, 0, c)
            if before:
                quantize(("w",) + before + (0,))
                quantize(("feature", before[0], 0, before[1]))
            weave(on_vector, ("w", a, c, 0))
            weave(on_scalar, ("w", a, c, 1))
            if c == 1:
                scale_mean(1 - a, a)
            if before:
                quantize(("w",) + before + (1,))
                for t, n, index in early:
                    dx_pass(0, t, n, before, index)
            if a == 1:
                load_x(c)
        quantize(("feature", 1, 0, 1))
        quantize(("w", 1, 1, 0))
        for t, n, index in early[:4]:
            dx_pass(0, t, n, steps[-1], index)

        make_dy(0, 1, 0)
        quantize(("w", 1, 1, 1))
        turn(0, 1, 0)
        for t, n, index in early[4:]:
            dx_pass(0, t, n, steps[-1], index)
        copy_out(on_scalar, ("dx", 0, 0), 0)
        copy_out(on_scalar, ("dx", 0, 1), 0)
        drain(0, 1, 0)

        make_dy(0, 1, 1)
        scale_mean(1, 1)
        turn(0, 1, 1)
        dx_group(0, 2, 1, 4)
        copy_out(on_scalar, ("dx", 0, 2), 0)
        copy_out(on_scalar, ("dx", 0, 3), 0)
        drain(0, 1, 1)

        make_dy(1, 1, 0)
        quantize(("feature", 0, 1, 0))
        turn(1, 1, 0)
        dx_group(0, 3, 1, 5)
        copy_out(on_scalar, ("dx", 0, 0), 1)
        copy_out(on_scalar, ("dx", 0, 1), 1)
        drain(1, 1, 0)

        make_dy(1, 1, 1)
        turn(1, 1, 1)
        copy_out(on_scalar, ("dx", 0, 2), 1)
        copy_out(on_scalar, ("dx", 0, 3), 1)
        drain(1, 1, 1)
        for t in range(T):
            store_dx(0, t)

        weave(on_vector, ("x", 0, 0))
        weave(on_scalar, ("x", 0, 1))
        quantize(("feature", 0, 1, 1))
        weave(on_vector, ("token", 0, 0, 0))
        quantize(("feature", 1, 1, 0))
        weave(on_vector, ("token", 0, 1, 0))
        quantize(("feature", 1, 1, 1))
        quantize(("token", 0, 0, 0))

        order = [6, 7, 2, 3, 4, 5, 0, 1]
        late = [(t, n, order[2 * t + n]) for t in range(T) for n in range(2)]
        for step in steps:
            for t, n, index in late[:4]:
                dx_pass(1, t, n, step, index)
        for t, n, index in late[4:]:
            dx_group(1, t, n, index)
        for t in range(T):
            copy_out(on_scalar, ("dx", 1, t), 0)
            copy_out(on_scalar, ("dx", 1, t), 1)
            store_dx(1, t)

        weave(on_vector, ("x", 1, 0))
        quantize(("x", 0, 0))
        weave(on_vector, ("x", 1, 1))
        quantize(("token", 0, 1, 0))
        quantize(("x", 1, 0))
        quantize(("x", 0, 1))
        quantize(("x", 1, 1))

        tokens = [("token", a, g, c) for a, c in steps for g in range(2)]
        weave(on_vector, tokens[2])
        for i, (a, c) in enumerate(steps):
            for k in range(2 * i + 2, min(2 * i + 4, len(tokens))):
                if k + 1 < len(tokens):
                    weave(on_vector, tokens[k + 1])
                quantize(tokens[k])
            for m in range(HEADS * c, HEADS * (c + 1)):
                shared = (a, m) >= SHARED_FROM
                for n in range(2):
                    dw_group(a, m, n, order[(2 * m + n) % len(order)])
                    copy_out(on_vector if shared and n == 1 else on_scalar, ("dw", a, m), n)
                if (a, m) == (1, H - 1):
                    store_dw(a, m, slice(0, N))
                    store_dw(a, m, slice(N, E))
                else:
                    store_dw(a, m, slice(0, E))
